import numpy as np
import ml_dtypes


def mxq(x, axis, fmt="e4m3"):
    dtype, down = {"e4m3": (ml_dtypes.float8_e4m3fn, 7), "e5m2": (ml_dtypes.float8_e5m2, 14)}[fmt]
    v = np.moveaxis(np.asarray(x, np.float32).astype(ml_dtypes.bfloat16).astype(np.float64), axis, -1)
    blocks = v.reshape(v.shape[:-1] + (-1, 32))
    amax = np.abs(blocks).max(-1, keepdims=True)
    byte = np.maximum(np.where(amax > 0, np.frexp(amax)[1] - 1 + 127, 0) - down, 1)
    scale = np.exp2(byte - 127.0)
    codes = (blocks / scale).astype(np.float32).astype(dtype).astype(np.float64)
    return np.moveaxis((codes * scale).reshape(v.shape), -1, axis)


WIDE = False


def mx_kscale(k):
    if not WIDE:
        return np.ones(k)
    levels = np.array([10, -10, 5, -5, 0])
    if k % 512:
        return np.exp2(np.random.permutation(np.resize(levels, k // 32))).repeat(32)
    a = np.empty((k // 512, 16))
    for p in range(k // 512):
        a[p, :8] = np.random.permutation(np.resize(levels, 8))
        for g in range(8):
            far = levels[np.abs(levels - a[p, g]) >= 10]
            a[p, g + 8] = far[np.random.randint(len(far))]
    return np.exp2(a.ravel()).repeat(32)


BF16 = ml_dtypes.bfloat16


def bf(x):
    return np.asarray(x, np.float32).astype(BF16)


def f64(x):
    return np.asarray(x).astype(np.float64)


B, S, D, H, NS = 8, 512, 512, 4, 3
DH = D // H


def heads(x):
    return x.reshape(B, S, H, DH).transpose(0, 2, 1, 3)


def setup_inputs():
    s = mx_kscale(D)

    def stream():
        return bf(np.random.standard_normal((B, S, D)) * s)

    def weight():
        return bf(np.random.standard_normal((D, D)) / np.sqrt(D) / s[:, None])

    def bias():
        return bf(np.random.standard_normal(D) * 0.1)

    w = (0.4 + 0.3 * np.random.random((NS, NS))) * np.sign(np.random.standard_normal((NS, NS)))
    return {"input_tensor": stream(), "position_embedding": stream(), "attr": stream(),
            "Wq": weight(), "bq": bias(), "Wqp": weight(), "bqp": bias(), "Wqa": weight(), "bqa": bias(),
            "w_matrix": bf(w)}


def reference(input_tensor, position_embedding, attr, Wq, bq, Wqp, bqp, Wqa, bqa, w_matrix):
    Qi = heads((mxq(f64(input_tensor), 2, "e4m3") @ mxq(f64(Wq), 0, "e4m3")) + f64(bq))
    Qp = heads((mxq(f64(position_embedding), 2, "e4m3") @ mxq(f64(Wqp), 0, "e4m3")) + f64(bqp))
    Qa = heads((mxq(f64(attr), 2, "e4m3") @ mxq(f64(Wqa), 0, "e4m3")) + f64(bqa))
    w = f64(w_matrix)
    Q_ki = w[0, 0] * Qi + w[1, 0] * Qp + w[2, 0] * Qa
    Q_kp = w[0, 1] * Qi + w[1, 1] * Qp + w[2, 1] * Qa
    Q_ka = w[0, 2] * Qi + w[1, 2] * Qp + w[2, 2] * Qa
    return Q_ki, Q_kp, Q_ka

@@ -1,0 +1,223 @@
+from contextlib import ExitStack
+
+import concourse.mybir as mybir
+from concourse.masks import make_identity
+
+F32 = mybir.dt.float32
+BF16 = mybir.dt.bfloat16
+U32 = mybir.dt.uint32
+U8 = mybir.dt.uint8
+FP8X4 = mybir.dt.float8_e4m3fn_x4
+MULT = mybir.AluOpType.mult
+ADD = mybir.AluOpType.add
+COPY = mybir.ActivationFunctionType.Copy
+
+P = 128
+PACK = 4
+NB, S, D, H, NS = 8, 512, 512, 4, 3
+DH = D // H
+TILES = S // P
+WORDS = D // 2
+AHEAD = 3
+
+FLOPS = 2 * NS * NB * S * D * D
+
+
+def tile_crossmultiheadattention_pa_t_kernel(
+    tc,
+    input_tensor,
+    position_embedding,
+    attr,
+    Wq,
+    bq,
+    Wqp,
+    bqp,
+    Wqa,
+    bqa,
+    w_matrix,
+    out_0,
+    out_1,
+    out_2,
+):
+    nc = tc.nc
+    streams = (input_tensor, position_embedding, attr)
+    weights = (Wq, Wqp, Wqa)
+    biases = (bq, bqp, bqa)
+    outs = (out_0, out_1, out_2)
+
+    with ExitStack() as ctx:
+        const = ctx.enter_context(tc.tile_pool(name="const", bufs=1))
+        x_pool = ctx.enter_context(tc.tile_pool(name="x", bufs=AHEAD))
+        grouped_pool = ctx.enter_context(tc.tile_pool(name="grouped", bufs=NS))
+        mx_pool = ctx.enter_context(tc.tile_pool(name="mx", bufs=2))
+        first_pool = ctx.enter_context(tc.tile_pool(name="first", bufs=2 * NS))
+        out_pool = ctx.enter_context(tc.tile_pool(name="out", bufs=3))
+        psum = ctx.enter_context(tc.psum_pool(name="psum", bufs=2))
+
+        x_raw = {}
+        x_grouped = {}
+        x_codes = {}
+        x_scales = {}
+        acc = {}
+
+        def load_stream(b, i):
+            raw = x_pool.tile([P, TILES * D], BF16, tag="x%d" % i, name="x%d" % i)
+            nc.sync.dma_start(out=raw[:], in_=streams[i][b].rearrange("(p j) k -> p (j k)", j=TILES))
+            x_raw[(b, i)] = raw
+
+        def transpose_stream(b, i):
+            words = x_raw[(b, i)][:].bitcast(F32)
+            grouped = grouped_pool.tile([P, S * PACK], BF16, tag="grouped", name="grouped", align_bytes=64)
+            grouped_words = grouped[:].bitcast(F32)
+            for half in range(2):
+                xt = psum.tile([P, 4 * P], F32, tag="xt", name="xt")
+                for jj in range(2):
+                    for u in range(2):
+                        first_word = (2 * half + jj) * WORDS + u
+                        nc.tensor.transpose(
+                            out=xt[:, (2 * jj + u) * P : (2 * jj + u + 1) * P],
+                            in_=words[:, first_word : (2 * half + jj + 1) * WORDS : 2],
+                            identity=ident[:],
+                        )
+                nc.scalar.copy(
+                    out=grouped_words[:, half * 4 * P : (half + 1) * 4 * P].rearrange(
+                        "q (jj r u) -> q jj r u", jj=2, u=2
+                    ),
+                    in_=xt[:].rearrange("q (jj u r) -> q jj r u", jj=2, u=2),
+                )
+            x_grouped[(b, i)] = grouped
+
+        def quantise_stream(b, i):
+            codes = mx_pool.tile([P, S], U32, tag="codes%d" % i, name="codes%d" % i, align_bytes=64)
+            scales = mx_pool.tile([P, S], U8, tag="scales%d" % i, name="scales%d" % i, align_bytes=64)
+            nc.vector.quantize_mx(out=codes[:].bitcast(FP8X4), scales=scales[:], in_=x_grouped[(b, i)][:])
+            x_codes[(b, i)] = codes
+            x_scales[(b, i)] = scales
+
+        def by_head(ap):
+            return ap.rearrange("p (h c) -> p h c", h=H)
+
+        def mix_tile(b, j):
+            tokens = slice(j * P, (j + 1) * P)
+            q = []
+            for i in range(NS):
+                q_i = psum.tile([P, D], F32, tag="q%d" % i, name="q%d" % i)
+                nc.tensor.matmul_mx(
+                    out=q_i[:],
+                    lhsT=x_codes[(b, i)][:, tokens].bitcast(FP8X4),
+                    lhsT_scale=x_scales[(b, i)][:, tokens],
+                    rhs=w_codes[i][:].bitcast(FP8X4),
+                    rhs_scale=w_scales[i][:],
+                    start=True,
+                    stop=True,
+                )
+                q.append(q_i)
+            first = []
+            for o in range(NS):
+                first_o = first_pool.tile([P, D], F32, tag="first", name="first")
+                nc.scalar.activation(out=first_o[:], in_=q[0][:], func=COPY, scale=w_all[:, o : o + 1])
+                first.append(first_o)
+            for o in range(NS):
+                nc.vector.scalar_tensor_tensor(
+                    out=acc[(b, o)][:, :, j, :],
+                    in0=by_head(q[1][:]),
+                    scalar=w_all[:, NS + o : NS + o + 1],
+                    in1=by_head(beta[o][:]),
+                    op0=MULT,
+                    op1=ADD,
+                )
+            for o in range(NS):
+                nc.vector.scalar_tensor_tensor(
+                    out=acc[(b, o)][:, :, j, :],
+                    in0=by_head(q[2][:]),
+                    scalar=w_all[:, 2 * NS + o : 2 * NS + o + 1],
+                    in1=acc[(b, o)][:, :, j, :],
+                    op0=MULT,
+                    op1=ADD,
+                )
+            for o in range(NS):
+                nc.gpsimd.tensor_tensor(
+                    out=acc[(b, o)][:, :, j, :],
+                    in0=acc[(b, o)][:, :, j, :],
+                    in1=by_head(first[o][:]),
+                    op=ADD,
+                )
+
+        ident = const.tile([P, P], F32, name="ident")
+        make_identity(nc, ident[:])
+
+        w_bf = const.tile([P, NS * NS], BF16, name="w_bf")
+        nc.scalar.dma_start(out=w_bf[:], in_=w_matrix.rearrange("i o -> (i o)").partition_broadcast(P))
+        w_all = const.tile([P, NS * NS], F32, name="w_all")
+        nc.vector.tensor_copy(out=w_all[:], in_=w_bf[:])
+
+        w_rows = const.tile([P, NS], BF16, name="w_rows")
+        nc.vector.memset(w_rows[:], 0.0)
+        nc.scalar.dma_start(out=w_rows[0:NS, :], in_=w_matrix)
+        bias_rows = const.tile([P, D], BF16, name="bias_rows")
+        nc.vector.memset(bias_rows[:], 0.0)
+        for i in range(NS):
+            nc.scalar.dma_start(out=bias_rows[i : i + 1, :], in_=biases[i].rearrange("(o c) -> o c", o=1))
+
+        w_raw = []
+        for i in range(NS):
+            raw = const.tile([P, PACK, D], BF16, name="w_raw%d" % i)
+            nc.sync.dma_start(
+                out=raw[:].rearrange("q t n -> q (t n)"),
+                in_=weights[i].rearrange("(q t) n -> q (t n)", t=PACK),
+            )
+            w_raw.append(raw)
+            load_stream(0, i)
+        for b in range(1, AHEAD):
+            for i in range(NS):
+                load_stream(b, i)
+
+        w_codes = []
+        w_scales = []
+        for i in range(NS):
+            grouped = const.tile([P, D, PACK], BF16, name="w_grouped%d" % i, align_bytes=64)
+            nc.vector.tensor_copy(out=grouped[:], in_=w_raw[i][:].rearrange("q t n -> q n t"))
+            codes = const.tile([P, D], U32, name="w_codes%d" % i, align_bytes=64)
+            scales = const.tile([P, D], U8, name="w_scales%d" % i, align_bytes=64)
+            nc.vector.quantize_mx(
+                out=codes[:].bitcast(FP8X4), scales=scales[:], in_=grouped[:].rearrange("q n t -> q (n t)")
+            )
+            w_codes.append(codes)
+            w_scales.append(scales)
+
+        beta = []
+        for o in range(NS):
+            beta_ps = psum.tile([P, D], F32, tag="q%d" % o, name="beta_ps")
+            nc.tensor.matmul(
+                out=beta_ps[:],
+                lhsT=w_rows[:, o : o + 1].to_broadcast([P, P]),
+                rhs=bias_rows[:],
+                start=True,
+                stop=True,
+            )
+            beta_o = const.tile([P, D], F32, name="beta%d" % o)
+            nc.scalar.copy(out=beta_o[:], in_=beta_ps[:])
+            beta.append(beta_o)
+
+        for i in range(NS):
+            transpose_stream(0, i)
+        for i in range(NS):
+            quantise_stream(0, i)
+
+        for b in range(NB):
+            if b + AHEAD < NB:
+                for i in range(NS):
+                    load_stream(b + AHEAD, i)
+            for o in range(NS):
+                acc[(b, o)] = out_pool.tile([P, H, TILES, DH], F32, tag="out%d" % o, name="out%d" % o)
+            for j in range(TILES):
+                if b + 1 < NB and j < NS:
+                    transpose_stream(b + 1, j)
+                if b + 1 < NB and j >= 1:
+                    quantise_stream(b + 1, j - 1)
+                mix_tile(b, j)
+            for o in range(NS):
+                nc.sync.dma_start(
+                    out=outs[o][b].rearrange("h (p j) c -> p h (j c)", j=TILES),
+                    in_=acc[(b, o)][:].rearrange("p h j c -> p h (j c)"),
+                )

@@ -11,13 +11,16 @@ FP8X4 = mybir.dt.float8_e4m3fn_x4
 MULT = mybir.AluOpType.mult
 ADD = mybir.AluOpType.add
 COPY = mybir.ActivationFunctionType.Copy
+IDENTITY = mybir.ActivationFunctionType.Identity
 
 P = 128
 PACK = 4
 NB, S, D, H, NS = 8, 512, 512, 4, 3
 DH = D // H
 TILES = S // P
+STEPS = NB * TILES
 WORDS = D // 2
+CB = D // P
 AHEAD = 3
 
 FLOPS = 2 * NS * NB * S * D * D
@@ -49,43 +52,55 @@ def tile_crossmultiheadattention_pa_t_kernel(
         const = ctx.enter_context(tc.tile_pool(name="const", bufs=1))
         x_pool = ctx.enter_context(tc.tile_pool(name="x", bufs=AHEAD))
         grouped_pool = ctx.enter_context(tc.tile_pool(name="grouped", bufs=NS))
-        mx_pool = ctx.enter_context(tc.tile_pool(name="mx", bufs=2))
-        first_pool = ctx.enter_context(tc.tile_pool(name="first", bufs=2 * NS))
-        out_pool = ctx.enter_context(tc.tile_pool(name="out", bufs=3))
-        psum = ctx.enter_context(tc.psum_pool(name="psum", bufs=2))
+        mx_pool = ctx.enter_context(tc.tile_pool(name="mx", bufs=3))
+        ft_pool = ctx.enter_context(tc.tile_pool(name="ft", bufs=2))
+        s1_pool = ctx.enter_context(tc.tile_pool(name="s1", bufs=3))
+        out_pool = ctx.enter_context(tc.tile_pool(name="out", bufs=2))
+        misc_ps = ctx.enter_context(tc.psum_pool(name="misc_ps", bufs=3))
+        q2_ps = ctx.enter_context(tc.psum_pool(name="q2_ps", bufs=2))
+        f_ps = ctx.enter_context(tc.psum_pool(name="f_ps", bufs=3))
 
         x_raw = {}
         x_grouped = {}
         x_codes = {}
         x_scales = {}
+        f_t = {}
+        s_1 = {}
+        q_2 = {}
+        f_bank = {}
         acc = {}
 
-        def load_stream(b, i):
+        def load_stream(b, i, parts=1):
             raw = x_pool.tile([P, TILES * D], BF16, tag="x%d" % i, name="x%d" % i)
-            nc.sync.dma_start(out=raw[:], in_=streams[i][b].rearrange("(p j) k -> p (j k)", j=TILES))
+            w = TILES * D // parts
+            src = streams[i][b].rearrange("(p j) k -> p (j k)", j=TILES)
+            for c in range(parts):
+                nc.sync.dma_start(out=raw[:, c * w : (c + 1) * w], in_=src[:, c * w : (c + 1) * w])
             x_raw[(b, i)] = raw
 
-        def transpose_stream(b, i):
+        def transpose_stream(b, k):
+            i, half = divmod(k, 2)
             words = x_raw[(b, i)][:].bitcast(F32)
-            grouped = grouped_pool.tile([P, S * PACK], BF16, tag="grouped", name="grouped", align_bytes=64)
-            grouped_words = grouped[:].bitcast(F32)
-            for half in range(2):
-                xt = psum.tile([P, 4 * P], F32, tag="xt", name="xt")
-                for jj in range(2):
-                    for u in range(2):
-                        first_word = (2 * half + jj) * WORDS + u
-                        nc.tensor.transpose(
-                            out=xt[:, (2 * jj + u) * P : (2 * jj + u + 1) * P],
-                            in_=words[:, first_word : (2 * half + jj + 1) * WORDS : 2],
-                            identity=ident[:],
-                        )
-                nc.scalar.copy(
-                    out=grouped_words[:, half * 4 * P : (half + 1) * 4 * P].rearrange(
-                        "q (jj r u) -> q jj r u", jj=2, u=2
-                    ),
-                    in_=xt[:].rearrange("q (jj u r) -> q jj r u", jj=2, u=2),
+            if half == 0:
+                x_grouped[(b, i)] = grouped_pool.tile(
+                    [P, S * PACK], BF16, tag="grouped", name="grouped", align_bytes=64
                 )
-            x_grouped[(b, i)] = grouped
+            grouped_words = x_grouped[(b, i)][:].bitcast(F32)
+            xt = misc_ps.tile([P, 4 * P], F32, tag="misc", name="xt")
+            for jj in range(2):
+                for u in range(2):
+                    row = (2 * half + jj) * WORDS
+                    nc.tensor.transpose(
+                        out=xt[:, (2 * jj + u) * P : (2 * jj + u + 1) * P],
+                        in_=words[:, row + u : row + WORDS : 2],
+                        identity=ident[:],
+                    )
+            nc.scalar.copy(
+                out=grouped_words[:, half * 4 * P : (half + 1) * 4 * P].rearrange(
+                    "q (jj r u) -> q jj r u", jj=2, u=2
+                ),
+                in_=xt[:].rearrange("q (jj u r) -> q jj r u", jj=2, u=2),
+            )
 
         def quantise_stream(b, i):
             codes = mx_pool.tile([P, S], U32, tag="codes%d" % i, name="codes%d" % i, align_bytes=64)
@@ -94,53 +109,109 @@ def tile_crossmultiheadattention_pa_t_kernel(
             x_codes[(b, i)] = codes
             x_scales[(b, i)] = scales
 
+        def project_across(b, cb, vector=False):
+            if cb == 0:
+                for o in range(NS):
+                    f_t[(b, o)] = ft_pool.tile([P, CB, S], F32, tag="ft%d" % o, name="ft%d" % o)
+            chans = slice(cb * P, (cb + 1) * P)
+            q0 = misc_ps.tile([P, S], F32, tag="misc", name="q0")
+            nc.tensor.matmul_mx(
+                out=q0[:],
+                lhsT=w_codes[0][:, chans].bitcast(FP8X4),
+                lhsT_scale=w_scales[0][:, chans],
+                rhs=x_codes[(b, 0)][:].bitcast(FP8X4),
+                rhs_scale=x_scales[(b, 0)][:],
+                start=True,
+                stop=True,
+            )
+            for o in range(NS):
+                if vector:
+                    nc.vector.tensor_scalar(
+                        out=f_t[(b, o)][:, cb, :],
+                        in0=q0[:],
+                        scalar1=w_all[:, o : o + 1],
+                        scalar2=beta[:, NS * cb + o : NS * cb + o + 1],
+                        op0=MULT,
+                        op1=ADD,
+                    )
+                else:
+                    nc.scalar.activation(
+                        out=f_t[(b, o)][:, cb, :],
+                        in_=q0[:],
+                        func=IDENTITY,
+                        bias=beta[:, NS * cb + o : NS * cb + o + 1],
+                        scale=w_all[:, o : o + 1],
+                    )
+
+        def project(s, i, q):
+            b, j = divmod(s, TILES)
+            tokens = slice(j * P, (j + 1) * P)
+            nc.tensor.matmul_mx(
+                out=q[:],
+                lhsT=x_codes[(b, i)][:, tokens].bitcast(FP8X4),
+                lhsT_scale=x_scales[(b, i)][:, tokens],
+                rhs=w_codes[i][:].bitcast(FP8X4),
+                rhs_scale=w_scales[i][:],
+                start=True,
+                stop=True,
+            )
+
+        def project_first(s):
+            q1 = misc_ps.tile([P, D], F32, tag="misc", name="q1")
+            project(s, 1, q1)
+            s1 = s1_pool.tile([P, D], F32, tag="s1", name="s1")
+            nc.scalar.copy(out=s1[:], in_=q1[:])
+            s_1[s] = s1
+
+        def project_last(s):
+            q2 = q2_ps.tile([P, D], F32, tag="q2", name="q2")
+            project(s, 2, q2)
+            q_2[s] = q2
+
+        def transpose_back(s):
+            b, j = divmod(s, TILES)
+            for o in range(NS):
+                bank = f_ps.tile([P, D], F32, tag="f", name="f")
+                for cb in range(CB):
+                    nc.tensor.transpose(
+                        out=bank[:, cb * P : (cb + 1) * P],
+                        in_=f_t[(b, o)][:, cb, j * P : (j + 1) * P],
+                        identity=ident[:],
+                    )
+                f_bank[(s, o)] = bank
+
         def by_head(ap):
             return ap.rearrange("p (h c) -> p h c", h=H)
 
-        def mix_tile(b, j):
-            tokens = slice(j * P, (j + 1) * P)
-            q = []
-            for i in range(NS):
-                q_i = psum.tile([P, D], F32, tag="q%d" % i, name="q%d" % i)
-                nc.tensor.matmul_mx(
-                    out=q_i[:],
-                    lhsT=x_codes[(b, i)][:, tokens].bitcast(FP8X4),
-                    lhsT_scale=x_scales[(b, i)][:, tokens],
-                    rhs=w_codes[i][:].bitcast(FP8X4),
-                    rhs_scale=w_scales[i][:],
-                    start=True,
-                    stop=True,
-                )
-                q.append(q_i)
-            first = []
-            for o in range(NS):
-                first_o = first_pool.tile([P, D], F32, tag="first", name="first")
-                nc.scalar.activation(out=first_o[:], in_=q[0][:], func=COPY, scale=w_all[:, o : o + 1])
-                first.append(first_o)
+        def mix_first(s):
+            b, j = divmod(s, TILES)
             for o in range(NS):
                 nc.vector.scalar_tensor_tensor(
                     out=acc[(b, o)][:, :, j, :],
-                    in0=by_head(q[1][:]),
+                    in0=by_head(s_1[s][:]),
                     scalar=w_all[:, NS + o : NS + o + 1],
-                    in1=by_head(beta[o][:]),
+                    in1=by_head(f_bank[(s, o)][:]),
                     op0=MULT,
                     op1=ADD,
                 )
+
+        def mix_last(s):
+            b, j = divmod(s, TILES)
             for o in range(NS):
                 nc.vector.scalar_tensor_tensor(
                     out=acc[(b, o)][:, :, j, :],
-                    in0=by_head(q[2][:]),
+                    in0=by_head(q_2[s][:]),
                     scalar=w_all[:, 2 * NS + o : 2 * NS + o + 1],
                     in1=acc[(b, o)][:, :, j, :],
                     op0=MULT,
                     op1=ADD,
                 )
+
+        def store(b, j0, j1):
             for o in range(NS):
-                nc.gpsimd.tensor_tensor(
-                    out=acc[(b, o)][:, :, j, :],
-                    in0=acc[(b, o)][:, :, j, :],
-                    in1=by_head(first[o][:]),
-                    op=ADD,
+                nc.sync.dma_start(
+                    out=outs[o][b].rearrange("h (p j) c -> p h j c", j=TILES)[:, :, j0:j1, :],
+                    in_=acc[(b, o)][:, :, j0:j1, :],
                 )
 
         ident = const.tile([P, P], F32, name="ident")
@@ -149,7 +220,6 @@ def tile_crossmultiheadattention_pa_t_kernel(
         w_bf = const.tile([P, NS * NS], BF16, name="w_bf")
         nc.scalar.dma_start(out=w_bf[:], in_=w_matrix.rearrange("i o -> (i o)").partition_broadcast(P))
         w_all = const.tile([P, NS * NS], F32, name="w_all")
-        nc.vector.tensor_copy(out=w_all[:], in_=w_bf[:])
 
         w_rows = const.tile([P, NS], BF16, name="w_rows")
         nc.vector.memset(w_rows[:], 0.0)
@@ -161,63 +231,150 @@ def tile_crossmultiheadattention_pa_t_kernel(
 
         w_raw = []
         for i in range(NS):
+            load_stream(0, i, parts=2 if i == 0 else 1)
             raw = const.tile([P, PACK, D], BF16, name="w_raw%d" % i)
             nc.sync.dma_start(
                 out=raw[:].rearrange("q t n -> q (t n)"),
                 in_=weights[i].rearrange("(q t) n -> q (t n)", t=PACK),
             )
             w_raw.append(raw)
-            load_stream(0, i)
         for b in range(1, AHEAD):
             for i in range(NS):
                 load_stream(b, i)
 
+        nc.vector.tensor_copy(out=w_all[:], in_=w_bf[:])
+        beta_ps = misc_ps.tile([P, CB * NS], F32, tag="misc", name="beta_ps")
+        for cb in range(CB):
+            nc.tensor.matmul(
+                out=beta_ps[:, NS * cb : NS * (cb + 1)],
+                lhsT=bias_rows[:, cb * P : (cb + 1) * P],
+                rhs=w_rows[:],
+                start=True,
+                stop=True,
+            )
+        beta = const.tile([P, CB * NS], F32, name="beta")
+        nc.scalar.copy(out=beta[:], in_=beta_ps[:])
+
+        w_grouped = []
         w_codes = []
         w_scales = []
-        for i in range(NS):
+
+        def group_weight(i):
             grouped = const.tile([P, D, PACK], BF16, name="w_grouped%d" % i, align_bytes=64)
-            nc.vector.tensor_copy(out=grouped[:], in_=w_raw[i][:].rearrange("q t n -> q n t"))
+            if i >= 1:
+                nc.gpsimd.tensor_scalar(
+                    out=grouped[:],
+                    in0=w_raw[i][:].rearrange("q t n -> q n t"),
+                    scalar1=1.0,
+                    scalar2=0.0,
+                    op0=MULT,
+                    op1=ADD,
+                )
+            else:
+                nc.vector.tensor_copy(
+                    out=grouped[:].rearrange("q (c i) t -> q c t i", i=4),
+                    in_=w_raw[i][:].rearrange("q t (c i) -> q c t i", i=4),
+                )
+            w_grouped.append(grouped)
+
+        def quantise_weight(i):
             codes = const.tile([P, D], U32, name="w_codes%d" % i, align_bytes=64)
             scales = const.tile([P, D], U8, name="w_scales%d" % i, align_bytes=64)
             nc.vector.quantize_mx(
-                out=codes[:].bitcast(FP8X4), scales=scales[:], in_=grouped[:].rearrange("q n t -> q (n t)")
+                out=codes[:].bitcast(FP8X4), scales=scales[:], in_=w_grouped[i][:].rearrange("q n t -> q (n t)")
             )
             w_codes.append(codes)
             w_scales.append(scales)
 
-        beta = []
-        for o in range(NS):
-            beta_ps = psum.tile([P, D], F32, tag="q%d" % o, name="beta_ps")
-            nc.tensor.matmul(
-                out=beta_ps[:],
-                lhsT=w_rows[:, o : o + 1].to_broadcast([P, P]),
-                rhs=bias_rows[:],
-                start=True,
-                stop=True,
+        ctx.enter_context(
+            tc.manual_schedule(
+                engines={mybir.EngineType.PE, mybir.EngineType.Activation, mybir.EngineType.DVE}
             )
-            beta_o = const.tile([P, D], F32, name="beta%d" % o)
-            nc.scalar.copy(out=beta_o[:], in_=beta_ps[:])
-            beta.append(beta_o)
+        )
 
+        for k in range(4):
+            transpose_stream(0, k)
         for i in range(NS):
-            transpose_stream(0, i)
-        for i in range(NS):
-            quantise_stream(0, i)
+            group_weight(i)
+        quantise_weight(0)
+        quantise_stream(0, 0)
+        quantise_stream(0, 1)
+        for cb in range(CB):
+            project_across(0, cb, vector=cb % 2 == 1)
+            if cb == 1:
+                quantise_weight(1)
+        project_first(0)
+        transpose_back(0)
+        for k in range(4, 6):
+            transpose_stream(0, k)
+        project_first(1)
+        for k in range(2):
+            transpose_stream(1, k)
 
-        for b in range(NB):
-            if b + AHEAD < NB:
-                for i in range(NS):
-                    load_stream(b + AHEAD, i)
-            for o in range(NS):
-                acc[(b, o)] = out_pool.tile([P, H, TILES, DH], F32, tag="out%d" % o, name="out%d" % o)
-            for j in range(TILES):
-                if b + 1 < NB and j < NS:
-                    transpose_stream(b + 1, j)
-                if b + 1 < NB and j >= 1:
-                    quantise_stream(b + 1, j - 1)
-                mix_tile(b, j)
-            for o in range(NS):
-                nc.sync.dma_start(
-                    out=outs[o][b].rearrange("h (p j) c -> p h (j c)", j=TILES),
-                    in_=acc[(b, o)][:].rearrange("p h j c -> p h (j c)"),
-                )
+        across = {
+            0: [(1, 0)],
+            1: [(1, 1)],
+            2: [(1, 2), (1, 3)],
+            4: [(2, 0)],
+            5: [(2, 1), (2, 2)],
+            6: [(2, 3)],
+        }
+        flips = {
+            0: [(1, 2), (1, 3)],
+            1: [(1, 4), (1, 5)],
+            3: [(2, 0), (2, 1), (2, 2), (2, 3)],
+            4: [(2, 4), (2, 5)],
+            6: [(3, 0), (3, 1), (3, 2), (3, 3)],
+            7: [(3, 4), (3, 5)],
+        }
+        quants = {
+            0: [(0, 2), (1, 0)],
+            1: [(1, 1)],
+            2: [(1, 2)],
+            4: [(2, 0), (2, 1)],
+            5: [(2, 2)],
+            7: [(3, 0), (3, 1)],
+            8: [(3, 2)],
+        }
+
+        def plan(table, b, first, per_step, count):
+            for n in range(count):
+                table.setdefault(first + n // per_step, []).append((b, n))
+
+        plan(across, 3, 7, 1, CB)
+        for b in range(4, NB):
+            plan(flips, b, TILES * b - 7, 2, 2 * NS)
+            plan(quants, b, TILES * b - 6, 1, NS)
+            plan(across, b, TILES * b - 5, 1, CB)
+
+        for s in range(STEPS):
+            b, j = divmod(s, TILES)
+            if j == 0:
+                if b + AHEAD < NB:
+                    for i in range(NS):
+                        load_stream(b + AHEAD, i)
+                for o in range(NS):
+                    acc[(b, o)] = out_pool.tile([P, H, TILES, DH], F32, tag="out%d" % o, name="out%d" % o)
+            mix_first(s)
+            if s + 1 < STEPS:
+                transpose_back(s + 1)
+            for b2, k in flips.get(s, []):
+                transpose_stream(b2, k)
+            if s == 0:
+                quantise_weight(2)
+            for b2, i in quants.get(s, []):
+                quantise_stream(b2, i)
+            if s == 0:
+                project_last(0)
+            if s + 1 < STEPS:
+                project_last(s + 1)
+            if s + 2 < STEPS:
+                project_first(s + 2)
+            for b2, cb in across.get(s, []):
+                project_across(b2, cb)
+            mix_last(s)
+            if b + 1 < NB:
+                if j == TILES - 1:
+                    store(b, 0, TILES)
+            elif j % 2 == 1:
+                store(b, j - 1, j + 1)

@@ -55,6 +55,7 @@ def tile_crossmultiheadattention_pa_t_kernel(
         mx_pool = ctx.enter_context(tc.tile_pool(name="mx", bufs=3))
         ft_pool = ctx.enter_context(tc.tile_pool(name="ft", bufs=2))
         s1_pool = ctx.enter_context(tc.tile_pool(name="s1", bufs=3))
+        g_pool = ctx.enter_context(tc.tile_pool(name="g", bufs=4))
         out_pool = ctx.enter_context(tc.tile_pool(name="out", bufs=2))
         misc_ps = ctx.enter_context(tc.psum_pool(name="misc_ps", bufs=3))
         q2_ps = ctx.enter_context(tc.psum_pool(name="q2_ps", bufs=2))
@@ -69,6 +70,7 @@ def tile_crossmultiheadattention_pa_t_kernel(
         q_2 = {}
         f_bank = {}
         acc = {}
+        spare = {}
 
         def load_stream(b, i, parts=1):
             raw = x_pool.tile([P, TILES * D], BF16, tag="x%d" % i, name="x%d" % i)
@@ -195,9 +197,32 @@ def tile_crossmultiheadattention_pa_t_kernel(
                     op1=ADD,
                 )
 
+        def spare_outputs(s):
+            if s >= STEPS - 1:
+                return ()
+            if s >= STEPS - TILES - 1:
+                return (1, 2)
+            return () if s % TILES == 1 else (2,)
+
+        def spare_terms(s):
+            for o in spare_outputs(s):
+                g = g_pool.tile([P, D], F32, tag="g", name="g")
+                nc.scalar.activation(
+                    out=g[:], in_=q_2[s][:], func=COPY, scale=w_all[:, 2 * NS + o : 2 * NS + o + 1]
+                )
+                spare[(s, o)] = g
+
         def mix_last(s):
             b, j = divmod(s, TILES)
             for o in range(NS):
+                if (s, o) in spare:
+                    nc.gpsimd.tensor_tensor(
+                        out=acc[(b, o)][:, :, j, :],
+                        in0=acc[(b, o)][:, :, j, :],
+                        in1=by_head(spare[(s, o)][:]),
+                        op=ADD,
+                    )
+                    continue
                 nc.vector.scalar_tensor_tensor(
                     out=acc[(b, o)][:, :, j, :],
                     in0=by_head(q_2[s][:]),
@@ -355,6 +380,8 @@ def tile_crossmultiheadattention_pa_t_kernel(
                         load_stream(b + AHEAD, i)
                 for o in range(NS):
                     acc[(b, o)] = out_pool.tile([P, H, TILES, DH], F32, tag="out%d" % o, name="out%d" % o)
+            if s > 0:
+                spare_terms(s)
             mix_first(s)
             if s + 1 < STEPS:
                 transpose_back(s + 1)

@@ -337,12 +337,13 @@ def tile_crossmultiheadattention_pa_t_kernel(
             transpose_stream(1, k)
 
         across = {
-            0: [(1, 0)],
-            1: [(1, 1)],
+            1: [(1, 0), (1, 1)],
             2: [(1, 2), (1, 3)],
-            4: [(2, 0)],
-            5: [(2, 1), (2, 2)],
-            6: [(2, 3)],
+            5: [(2, 0), (2, 1)],
+            6: [(2, 2), (2, 3)],
+            8: [(3, 0)],
+            9: [(3, 1), (3, 2)],
+            10: [(3, 3)],
         }
         flips = {
             0: [(1, 2), (1, 3)],
@@ -353,7 +354,7 @@ def tile_crossmultiheadattention_pa_t_kernel(
             7: [(3, 4), (3, 5)],
         }
         quants = {
-            0: [(0, 2), (1, 0)],
+            0: [(1, 0)],
             1: [(1, 1)],
             2: [(1, 2)],
             4: [(2, 0), (2, 1)],
@@ -366,7 +367,6 @@ def tile_crossmultiheadattention_pa_t_kernel(
             for n in range(count):
                 table.setdefault(first + n // per_step, []).append((b, n))
 
-        plan(across, 3, 7, 1, CB)
         for b in range(4, NB):
             plan(flips, b, TILES * b - 7, 2, 2 * NS)
             plan(quants, b, TILES * b - 6, 1, NS)
@@ -380,25 +380,24 @@ def tile_crossmultiheadattention_pa_t_kernel(
                         load_stream(b + AHEAD, i)
                 for o in range(NS):
                     acc[(b, o)] = out_pool.tile([P, H, TILES, DH], F32, tag="out%d" % o, name="out%d" % o)
-            if s > 0:
-                spare_terms(s)
+            if s + 2 < STEPS:
+                project_first(s + 2)
+            for b2, cb in across.get(s, []):
+                project_across(b2, cb)
+            if s == 0:
+                quantise_weight(2)
+                quantise_stream(0, 2)
+                project_last(0)
+            if s + 1 < STEPS:
+                project_last(s + 1)
+                spare_terms(s + 1)
             mix_first(s)
             if s + 1 < STEPS:
                 transpose_back(s + 1)
             for b2, k in flips.get(s, []):
                 transpose_stream(b2, k)
-            if s == 0:
-                quantise_weight(2)
             for b2, i in quants.get(s, []):
                 quantise_stream(b2, i)
-            if s == 0:
-                project_last(0)
-            if s + 1 < STEPS:
-                project_last(s + 1)
-            if s + 2 < STEPS:
-                project_first(s + 2)
-            for b2, cb in across.get(s, []):
-                project_across(b2, cb)
             mix_last(s)
             if b + 1 < NB:
                 if j == TILES - 1:

@@ -55,6 +55,7 @@ def tile_crossmultiheadattention_pa_t_kernel(
         mx_pool = ctx.enter_context(tc.tile_pool(name="mx", bufs=3))
         ft_pool = ctx.enter_context(tc.tile_pool(name="ft", bufs=2))
         s1_pool = ctx.enter_context(tc.tile_pool(name="s1", bufs=3))
+        s0_pool = ctx.enter_context(tc.tile_pool(name="s0", bufs=3))
         g_pool = ctx.enter_context(tc.tile_pool(name="g", bufs=4))
         out_pool = ctx.enter_context(tc.tile_pool(name="out", bufs=2))
         misc_ps = ctx.enter_context(tc.psum_pool(name="misc_ps", bufs=3))
@@ -127,7 +128,19 @@ def tile_crossmultiheadattention_pa_t_kernel(
                 stop=True,
             )
             for o in range(NS):
-                if vector:
+                if not vector and b > 0 and o > 0:
+                    if o == 1:
+                        s0 = s0_pool.tile([P, S], F32, tag="s0", name="s0")
+                        nc.scalar.copy(out=s0[:], in_=q0[:])
+                    nc.gpsimd.tensor_scalar(
+                        out=f_t[(b, o)][:, cb, :],
+                        in0=s0[:],
+                        scalar1=w_all[:, o : o + 1],
+                        scalar2=beta[:, NS * cb + o : NS * cb + o + 1],
+                        op0=MULT,
+                        op1=ADD,
+                    )
+                elif vector:
                     nc.vector.tensor_scalar(
                         out=f_t[(b, o)][:, cb, :],
                         in0=q0[:],
@@ -202,7 +215,7 @@ def tile_crossmultiheadattention_pa_t_kernel(
                 return ()
             if s >= STEPS - TILES - 1:
                 return (1, 2)
-            return () if s % TILES == 1 else (2,)
+            return (1, 2) if s % TILES == 0 and s > 0 else (2,)
 
         def spare_terms(s):
             for o in spare_outputs(s):
@@ -286,20 +299,10 @@ def tile_crossmultiheadattention_pa_t_kernel(
 
         def group_weight(i):
             grouped = const.tile([P, D, PACK], BF16, name="w_grouped%d" % i, align_bytes=64)
-            if i >= 1:
-                nc.gpsimd.tensor_scalar(
-                    out=grouped[:],
-                    in0=w_raw[i][:].rearrange("q t n -> q n t"),
-                    scalar1=1.0,
-                    scalar2=0.0,
-                    op0=MULT,
-                    op1=ADD,
-                )
-            else:
-                nc.vector.tensor_copy(
-                    out=grouped[:].rearrange("q (c i) t -> q c t i", i=4),
-                    in_=w_raw[i][:].rearrange("q t (c i) -> q c t i", i=4),
-                )
+            nc.vector.tensor_copy(
+                out=grouped[:].rearrange("q (c i) t -> q c t i", i=4),
+                in_=w_raw[i][:].rearrange("q t (c i) -> q c t i", i=4),
+            )
             w_grouped.append(grouped)
 
         def quantise_weight(i):
@@ -319,19 +322,21 @@ def tile_crossmultiheadattention_pa_t_kernel(
 
         for k in range(4):
             transpose_stream(0, k)
-        for i in range(NS):
-            group_weight(i)
+        group_weight(0)
         quantise_weight(0)
         quantise_stream(0, 0)
+        group_weight(1)
+        project_across(0, 0)
+        project_across(0, 1, vector=True)
+        quantise_weight(1)
         quantise_stream(0, 1)
-        for cb in range(CB):
-            project_across(0, cb, vector=cb % 2 == 1)
-            if cb == 1:
-                quantise_weight(1)
+        project_across(0, 2)
+        transpose_stream(0, 4)
+        project_across(0, 3, vector=True)
         project_first(0)
         transpose_back(0)
-        for k in range(4, 6):
-            transpose_stream(0, k)
+        group_weight(2)
+        transpose_stream(0, 5)
         project_first(1)
         for k in range(2):
             transpose_stream(1, k)
@@ -339,35 +344,31 @@ def tile_crossmultiheadattention_pa_t_kernel(
         across = {
             1: [(1, 0), (1, 1)],
             2: [(1, 2), (1, 3)],
-            5: [(2, 0), (2, 1)],
-            6: [(2, 2), (2, 3)],
-            8: [(3, 0)],
-            9: [(3, 1), (3, 2)],
-            10: [(3, 3)],
+            4: [(2, 0)],
+            5: [(2, 1), (2, 2)],
+            6: [(2, 3)],
         }
         flips = {
             0: [(1, 2), (1, 3)],
             1: [(1, 4), (1, 5)],
-            3: [(2, 0), (2, 1), (2, 2), (2, 3)],
+            2: [(2, 0), (2, 1)],
+            3: [(2, 2), (2, 3)],
             4: [(2, 4), (2, 5)],
-            6: [(3, 0), (3, 1), (3, 2), (3, 3)],
-            7: [(3, 4), (3, 5)],
         }
         quants = {
             0: [(1, 0)],
             1: [(1, 1)],
             2: [(1, 2)],
-            4: [(2, 0), (2, 1)],
+            3: [(2, 0)],
+            4: [(2, 1)],
             5: [(2, 2)],
-            7: [(3, 0), (3, 1)],
-            8: [(3, 2)],
         }
 
         def plan(table, b, first, per_step, count):
             for n in range(count):
                 table.setdefault(first + n // per_step, []).append((b, n))
 
-        for b in range(4, NB):
+        for b in range(3, NB):
             plan(flips, b, TILES * b - 7, 2, 2 * NS)
             plan(quants, b, TILES * b - 6, 1, NS)
             plan(across, b, TILES * b - 5, 1, CB)
@@ -380,25 +381,30 @@ def tile_crossmultiheadattention_pa_t_kernel(
                         load_stream(b + AHEAD, i)
                 for o in range(NS):
                     acc[(b, o)] = out_pool.tile([P, H, TILES, DH], F32, tag="out%d" % o, name="out%d" % o)
-            if s + 2 < STEPS:
+            for b2, k in flips.get(s, [])[:2] if s else []:
+                transpose_stream(b2, k)
+            if 0 < s < STEPS - 2:
                 project_first(s + 2)
             for b2, cb in across.get(s, []):
                 project_across(b2, cb)
-            if s == 0:
-                quantise_weight(2)
-                quantise_stream(0, 2)
-                project_last(0)
-            if s + 1 < STEPS:
+            if 0 < s < STEPS - 1:
                 project_last(s + 1)
                 spare_terms(s + 1)
             mix_first(s)
             if s + 1 < STEPS:
                 transpose_back(s + 1)
-            for b2, k in flips.get(s, []):
+            if s == 0:
+                quantise_weight(2)
+                quantise_stream(0, 2)
+                project_last(0)
+                project_last(1)
+                spare_terms(1)
+                project_first(2)
+            for b2, k in flips.get(s, [])[2:] if s else flips[0]:
                 transpose_stream(b2, k)
+            mix_last(s)
             for b2, i in quants.get(s, []):
                 quantise_stream(b2, i)
-            mix_last(s)
             if b + 1 < NB:
                 if j == TILES - 1:
                     store(b, 0, TILES)

@@ -23,6 +23,8 @@ WORDS = D // 2
 CB = D // P
 AHEAD = 3
 
+TAIL = STEPS - 6
+
 FLOPS = 2 * NS * NB * S * D * D
 
 
@@ -55,7 +57,6 @@ def tile_crossmultiheadattention_pa_t_kernel(
         mx_pool = ctx.enter_context(tc.tile_pool(name="mx", bufs=3))
         ft_pool = ctx.enter_context(tc.tile_pool(name="ft", bufs=2))
         s1_pool = ctx.enter_context(tc.tile_pool(name="s1", bufs=3))
-        s0_pool = ctx.enter_context(tc.tile_pool(name="s0", bufs=3))
         g_pool = ctx.enter_context(tc.tile_pool(name="g", bufs=4))
         out_pool = ctx.enter_context(tc.tile_pool(name="out", bufs=2))
         misc_ps = ctx.enter_context(tc.psum_pool(name="misc_ps", bufs=3))
@@ -128,19 +129,7 @@ def tile_crossmultiheadattention_pa_t_kernel(
                 stop=True,
             )
             for o in range(NS):
-                if not vector and b > 0 and o > 0:
-                    if o == 1:
-                        s0 = s0_pool.tile([P, S], F32, tag="s0", name="s0")
-                        nc.scalar.copy(out=s0[:], in_=q0[:])
-                    nc.gpsimd.tensor_scalar(
-                        out=f_t[(b, o)][:, cb, :],
-                        in0=s0[:],
-                        scalar1=w_all[:, o : o + 1],
-                        scalar2=beta[:, NS * cb + o : NS * cb + o + 1],
-                        op0=MULT,
-                        op1=ADD,
-                    )
-                elif vector:
+                if vector:
                     nc.vector.tensor_scalar(
                         out=f_t[(b, o)][:, cb, :],
                         in0=q0[:],
@@ -211,30 +200,34 @@ def tile_crossmultiheadattention_pa_t_kernel(
                 )
 
         def spare_outputs(s):
-            if s >= STEPS - 1:
+            if s < 2 or s >= STEPS - 2:
                 return ()
-            if s >= STEPS - TILES - 1:
+            if s >= TAIL:
                 return (1, 2)
-            return (1, 2) if s % TILES == 0 and s > 0 else (2,)
+            return (2,) if s % TILES < 2 else ()
 
         def spare_terms(s):
             for o in spare_outputs(s):
-                g = g_pool.tile([P, D], F32, tag="g", name="g")
+                if s % 2 == 0:
+                    spare[(s // 2, o)] = g_pool.tile([P, 2, D], F32, tag="g", name="g")
                 nc.scalar.activation(
-                    out=g[:], in_=q_2[s][:], func=COPY, scale=w_all[:, 2 * NS + o : 2 * NS + o + 1]
+                    out=spare[(s // 2, o)][:, s % 2, :],
+                    in_=q_2[s][:],
+                    func=COPY,
+                    scale=w_all[:, 2 * NS + o : 2 * NS + o + 1],
                 )
-                spare[(s, o)] = g
 
         def mix_last(s):
             b, j = divmod(s, TILES)
             for o in range(NS):
-                if (s, o) in spare:
-                    nc.gpsimd.tensor_tensor(
-                        out=acc[(b, o)][:, :, j, :],
-                        in0=acc[(b, o)][:, :, j, :],
-                        in1=by_head(spare[(s, o)][:]),
-                        op=ADD,
-                    )
+                if o in spare_outputs(s):
+                    if s % 2 == 1:
+                        nc.gpsimd.tensor_tensor(
+                            out=acc[(b, o)][:, :, j - 1 : j + 1, :],
+                            in0=acc[(b, o)][:, :, j - 1 : j + 1, :],
+                            in1=spare[(s // 2, o)][:].rearrange("p j (h c) -> p h j c", h=H),
+                            op=ADD,
+                        )
                     continue
                 nc.vector.scalar_tensor_tensor(
                     out=acc[(b, o)][:, :, j, :],

@@ -23,7 +23,12 @@ WORDS = D // 2
 CB = D // P
 AHEAD = 3
 
-TAIL = STEPS - 6
+POOL_F = [(b, 0) for b in range(1, 7)]
+GB = 6
+G_FIRST = ()
+G_MID = ((2, 0, 2, 1), (1, 0, 1, 1))
+G_LATE = G_MID + ((1, 2, 4, 3), (2, 2, 4, 3))
+G_LAST = ((1, 0, 2, 1), (2, 0, 2, 1), (2, 2, 3, 2))
 
 FLOPS = 2 * NS * NB * S * D * D
 
@@ -57,7 +62,8 @@ def tile_crossmultiheadattention_pa_t_kernel(
         mx_pool = ctx.enter_context(tc.tile_pool(name="mx", bufs=3))
         ft_pool = ctx.enter_context(tc.tile_pool(name="ft", bufs=2))
         s1_pool = ctx.enter_context(tc.tile_pool(name="s1", bufs=3))
-        g_pool = ctx.enter_context(tc.tile_pool(name="g", bufs=4))
+        s0_pool = ctx.enter_context(tc.tile_pool(name="s0", bufs=3))
+        g_pool = ctx.enter_context(tc.tile_pool(name="g", bufs=GB))
         out_pool = ctx.enter_context(tc.tile_pool(name="out", bufs=2))
         misc_ps = ctx.enter_context(tc.psum_pool(name="misc_ps", bufs=3))
         q2_ps = ctx.enter_context(tc.psum_pool(name="q2_ps", bufs=2))
@@ -68,24 +74,23 @@ def tile_crossmultiheadattention_pa_t_kernel(
         x_codes = {}
         x_scales = {}
         f_t = {}
+        q_0 = {}
         s_1 = {}
         q_2 = {}
         f_bank = {}
         acc = {}
         spare = {}
 
-        def load_stream(b, i, parts=1):
-            raw = x_pool.tile([P, TILES * D], BF16, tag="x%d" % i, name="x%d" % i)
-            w = TILES * D // parts
+        def load_stream(b, i, cols=slice(0, TILES * D)):
+            if (b, i) not in x_raw:
+                x_raw[(b, i)] = x_pool.tile([P, TILES * D], BF16, tag="x%d" % i, name="x%d" % i)
             src = streams[i][b].rearrange("(p j) k -> p (j k)", j=TILES)
-            for c in range(parts):
-                nc.sync.dma_start(out=raw[:, c * w : (c + 1) * w], in_=src[:, c * w : (c + 1) * w])
-            x_raw[(b, i)] = raw
+            nc.sync.dma_start(out=x_raw[(b, i)][:, cols], in_=src[:, cols])
 
         def transpose_stream(b, k):
             i, half = divmod(k, 2)
             words = x_raw[(b, i)][:].bitcast(F32)
-            if half == 0:
+            if (b, i) not in x_grouped:
                 x_grouped[(b, i)] = grouped_pool.tile(
                     [P, S * PACK], BF16, tag="grouped", name="grouped", align_bytes=64
                 )
@@ -106,33 +111,52 @@ def tile_crossmultiheadattention_pa_t_kernel(
                 in_=xt[:].rearrange("q (jj u r) -> q jj r u", jj=2, u=2),
             )
 
-        def quantise_stream(b, i):
-            codes = mx_pool.tile([P, S], U32, tag="codes%d" % i, name="codes%d" % i, align_bytes=64)
-            scales = mx_pool.tile([P, S], U8, tag="scales%d" % i, name="scales%d" % i, align_bytes=64)
-            nc.vector.quantize_mx(out=codes[:].bitcast(FP8X4), scales=scales[:], in_=x_grouped[(b, i)][:])
-            x_codes[(b, i)] = codes
-            x_scales[(b, i)] = scales
-
-        def project_across(b, cb, vector=False):
-            if cb == 0:
-                for o in range(NS):
-                    f_t[(b, o)] = ft_pool.tile([P, CB, S], F32, tag="ft%d" % o, name="ft%d" % o)
-            chans = slice(cb * P, (cb + 1) * P)
-            q0 = misc_ps.tile([P, S], F32, tag="misc", name="q0")
-            nc.tensor.matmul_mx(
-                out=q0[:],
-                lhsT=w_codes[0][:, chans].bitcast(FP8X4),
-                lhsT_scale=w_scales[0][:, chans],
-                rhs=x_codes[(b, 0)][:].bitcast(FP8X4),
-                rhs_scale=x_scales[(b, 0)][:],
-                start=True,
-                stop=True,
+        def quantise_stream(b, i, tokens=slice(0, S)):
+            if (b, i) not in x_codes:
+                x_codes[(b, i)] = mx_pool.tile([P, S], U32, tag="codes%d" % i, name="codes%d" % i, align_bytes=64)
+                x_scales[(b, i)] = mx_pool.tile([P, S], U8, tag="scales%d" % i, name="scales%d" % i, align_bytes=64)
+            nc.vector.quantize_mx(
+                out=x_codes[(b, i)][:, tokens].bitcast(FP8X4),
+                scales=x_scales[(b, i)][:, tokens],
+                in_=x_grouped[(b, i)][:, tokens.start * PACK : tokens.stop * PACK],
             )
+
+        def project_across(b, blocks, tokens=slice(0, S)):
+            n = tokens.stop - tokens.start
+            q0 = misc_ps.tile([P, S], F32, tag="misc", name="q0")
+            for m, cb in enumerate(blocks):
+                chans = slice(cb * P, (cb + 1) * P)
+                nc.tensor.matmul_mx(
+                    out=q0[:, m * n : (m + 1) * n],
+                    lhsT=w_codes[0][:, chans].bitcast(FP8X4),
+                    lhsT_scale=w_scales[0][:, chans],
+                    rhs=x_codes[(b, 0)][:, tokens].bitcast(FP8X4),
+                    rhs_scale=x_scales[(b, 0)][:, tokens],
+                    start=True,
+                    stop=True,
+                )
+                q_0[(b, cb, tokens.start)] = q0[:, m * n : (m + 1) * n]
+
+        def scale_across(b, cb, tokens=slice(0, S), vector=False):
             for o in range(NS):
-                if vector:
+                if (b, o) not in f_t:
+                    f_t[(b, o)] = ft_pool.tile([P, CB, S], F32, tag="ft%d" % o, name="ft%d" % o)
+                if o > 0 and (b, cb) in POOL_F:
+                    if o == 1:
+                        s0 = s0_pool.tile([P, S], F32, tag="s0", name="s0")
+                        nc.scalar.copy(out=s0[:], in_=q_0[(b, cb, tokens.start)])
+                    nc.gpsimd.tensor_scalar(
+                        out=f_t[(b, o)][:, cb, tokens],
+                        in0=s0[:],
+                        scalar1=w_all[:, o : o + 1],
+                        scalar2=beta[:, NS * cb + o : NS * cb + o + 1],
+                        op0=MULT,
+                        op1=ADD,
+                    )
+                elif vector:
                     nc.vector.tensor_scalar(
-                        out=f_t[(b, o)][:, cb, :],
-                        in0=q0[:],
+                        out=f_t[(b, o)][:, cb, tokens],
+                        in0=q_0[(b, cb, tokens.start)],
                         scalar1=w_all[:, o : o + 1],
                         scalar2=beta[:, NS * cb + o : NS * cb + o + 1],
                         op0=MULT,
@@ -140,8 +164,8 @@ def tile_crossmultiheadattention_pa_t_kernel(
                     )
                 else:
                     nc.scalar.activation(
-                        out=f_t[(b, o)][:, cb, :],
-                        in_=q0[:],
+                        out=f_t[(b, o)][:, cb, tokens],
+                        in_=q_0[(b, cb, tokens.start)],
                         func=IDENTITY,
                         bias=beta[:, NS * cb + o : NS * cb + o + 1],
                         scale=w_all[:, o : o + 1],
@@ -199,19 +223,30 @@ def tile_crossmultiheadattention_pa_t_kernel(
                     op1=ADD,
                 )
 
-        def spare_outputs(s):
-            if s < 2 or s >= STEPS - 2:
-                return ()
-            if s >= TAIL:
-                return (1, 2)
-            return (2,) if s % TILES < 2 else ()
+        def spare_groups(b):
+            if b == 0:
+                return G_FIRST
+            if b < NB - 2:
+                return G_MID
+            return G_LATE if b == NB - 2 else G_LAST
+
+        def spare_group(s, o):
+            b, j = divmod(s, TILES)
+            for g in spare_groups(b):
+                if g[0] == o and g[1] <= j < g[2]:
+                    return g
+            return None
 
         def spare_terms(s):
-            for o in spare_outputs(s):
-                if s % 2 == 0:
-                    spare[(s // 2, o)] = g_pool.tile([P, 2, D], F32, tag="g", name="g")
+            b, j = divmod(s, TILES)
+            for o in range(NS):
+                g = spare_group(s, o)
+                if g is None:
+                    continue
+                if j == g[1]:
+                    spare[(b, g)] = g_pool.tile([P, 2, D], F32, tag="g", name="g")
                 nc.scalar.activation(
-                    out=spare[(s // 2, o)][:, s % 2, :],
+                    out=spare[(b, g)][:, j - g[1], :],
                     in_=q_2[s][:],
                     func=COPY,
                     scale=w_all[:, 2 * NS + o : 2 * NS + o + 1],
@@ -219,15 +254,17 @@ def tile_crossmultiheadattention_pa_t_kernel(
 
         def mix_last(s):
             b, j = divmod(s, TILES)
+            for g in spare_groups(b):
+                if g[3] == j:
+                    o, j0, j1 = g[:3]
+                    nc.gpsimd.tensor_tensor(
+                        out=acc[(b, o)][:, :, j0:j1, :],
+                        in0=acc[(b, o)][:, :, j0:j1, :],
+                        in1=spare[(b, g)][:, 0 : j1 - j0, :].rearrange("p j (h c) -> p h j c", h=H),
+                        op=ADD,
+                    )
             for o in range(NS):
-                if o in spare_outputs(s):
-                    if s % 2 == 1:
-                        nc.gpsimd.tensor_tensor(
-                            out=acc[(b, o)][:, :, j - 1 : j + 1, :],
-                            in0=acc[(b, o)][:, :, j - 1 : j + 1, :],
-                            in1=spare[(s // 2, o)][:].rearrange("p j (h c) -> p h j c", h=H),
-                            op=ADD,
-                        )
+                if spare_group(s, o) is not None:
                     continue
                 nc.vector.scalar_tensor_tensor(
                     out=acc[(b, o)][:, :, j, :],
@@ -261,30 +298,43 @@ def tile_crossmultiheadattention_pa_t_kernel(
             nc.scalar.dma_start(out=bias_rows[i : i + 1, :], in_=biases[i].rearrange("(o c) -> o c", o=1))
 
         w_raw = []
-        for i in range(NS):
-            load_stream(0, i, parts=2 if i == 0 else 1)
+
+        def load_weight(i):
             raw = const.tile([P, PACK, D], BF16, name="w_raw%d" % i)
             nc.sync.dma_start(
                 out=raw[:].rearrange("q t n -> q (t n)"),
                 in_=weights[i].rearrange("(q t) n -> q (t n)", t=PACK),
             )
             w_raw.append(raw)
+
+        first_half = slice(0, TILES * D // 2)
+        second_half = slice(TILES * D // 2, TILES * D)
+        load_stream(0, 0, first_half)
+        load_weight(0)
+        load_stream(0, 1, first_half)
+        load_weight(1)
+        load_stream(0, 0, second_half)
+        load_stream(0, 1, second_half)
+        load_stream(0, 2)
+        load_weight(2)
         for b in range(1, AHEAD):
             for i in range(NS):
                 load_stream(b, i)
 
         nc.vector.tensor_copy(out=w_all[:], in_=w_bf[:])
-        beta_ps = misc_ps.tile([P, CB * NS], F32, tag="misc", name="beta_ps")
-        for cb in range(CB):
-            nc.tensor.matmul(
-                out=beta_ps[:, NS * cb : NS * (cb + 1)],
-                lhsT=bias_rows[:, cb * P : (cb + 1) * P],
-                rhs=w_rows[:],
-                start=True,
-                stop=True,
-            )
         beta = const.tile([P, CB * NS], F32, name="beta")
-        nc.scalar.copy(out=beta[:], in_=beta_ps[:])
+
+        def mix_bias():
+            beta_ps = misc_ps.tile([P, CB * NS], F32, tag="misc", name="beta_ps")
+            for cb in range(CB):
+                nc.tensor.matmul(
+                    out=beta_ps[:, NS * cb : NS * (cb + 1)],
+                    lhsT=bias_rows[:, cb * P : (cb + 1) * P],
+                    rhs=w_rows[:],
+                    start=True,
+                    stop=True,
+                )
+            nc.scalar.copy(out=beta[:], in_=beta_ps[:])
 
         w_grouped = []
         w_codes = []
@@ -313,26 +363,28 @@ def tile_crossmultiheadattention_pa_t_kernel(
             )
         )
 
-        for k in range(4):
-            transpose_stream(0, k)
+        early = slice(0, S // 2)
+        late = slice(S // 2, S)
+        transpose_stream(0, 0)
+        mix_bias()
+        transpose_stream(0, 2)
         group_weight(0)
+        quantise_stream(0, 0, early)
         quantise_weight(0)
-        quantise_stream(0, 0)
+        project_across(0, (0, 2), early)
+        project_across(0, (1, 3), early)
         group_weight(1)
-        project_across(0, 0)
-        project_across(0, 1, vector=True)
+        quantise_stream(0, 1, early)
         quantise_weight(1)
-        quantise_stream(0, 1)
-        project_across(0, 2)
-        transpose_stream(0, 4)
-        project_across(0, 3, vector=True)
+        scale_across(0, 0, early)
+        scale_across(0, 2, early)
+        scale_across(0, 1, early, vector=True)
+        scale_across(0, 3, early, vector=True)
         project_first(0)
         transpose_back(0)
-        group_weight(2)
-        transpose_stream(0, 5)
         project_first(1)
-        for k in range(2):
-            transpose_stream(1, k)
+        for k in (1, 4, 5, 3):
+            transpose_stream(0, k)
 
         across = {
             1: [(1, 0), (1, 1)],
@@ -376,26 +428,39 @@ def tile_crossmultiheadattention_pa_t_kernel(
                     acc[(b, o)] = out_pool.tile([P, H, TILES, DH], F32, tag="out%d" % o, name="out%d" % o)
             for b2, k in flips.get(s, [])[:2] if s else []:
                 transpose_stream(b2, k)
-            if 0 < s < STEPS - 2:
-                project_first(s + 2)
-            for b2, cb in across.get(s, []):
-                project_across(b2, cb)
             if 0 < s < STEPS - 1:
                 project_last(s + 1)
                 spare_terms(s + 1)
+            if 0 < s < STEPS - 2:
+                project_first(s + 2)
+            for b2, cb in across.get(s, []):
+                project_across(b2, (cb,))
+                scale_across(b2, cb)
             mix_first(s)
             if s + 1 < STEPS:
                 transpose_back(s + 1)
             if s == 0:
+                group_weight(2)
+                quantise_stream(0, 0, late)
                 quantise_weight(2)
                 quantise_stream(0, 2)
+                project_across(0, (0, 2), late)
+                project_across(0, (1, 3), late)
                 project_last(0)
                 project_last(1)
                 spare_terms(1)
+                scale_across(0, 0, late)
+                scale_across(0, 2, late)
+                quantise_stream(0, 1, late)
                 project_first(2)
+                transpose_stream(1, 0)
+                transpose_stream(1, 1)
             for b2, k in flips.get(s, [])[2:] if s else flips[0]:
                 transpose_stream(b2, k)
             mix_last(s)
+            if s == 0:
+                scale_across(0, 1, late, vector=True)
+                scale_across(0, 3, late, vector=True)
             for b2, i in quants.get(s, []):
                 quantise_stream(b2, i)
             if b + 1 < NB:

@@ -23,7 +23,7 @@ WORDS = D // 2
 CB = D // P
 AHEAD = 3
 
-POOL_F = [(b, 0) for b in range(1, 7)]
+POOL_F = [(b, c) for b in range(1, NB) for c in (0, 1)]
 GB = 6
 G_FIRST = ()
 G_MID = ((2, 0, 2, 1), (1, 0, 1, 1))
@@ -466,5 +466,7 @@ def tile_crossmultiheadattention_pa_t_kernel(
             if b + 1 < NB:
                 if j == TILES - 1:
                     store(b, 0, TILES)
-            elif j % 2 == 1:
-                store(b, j - 1, j + 1)
+            elif j == 1:
+                store(b, 0, 2)
+            elif j >= 2:
+                store(b, j, j + 1)

@@ -213,7 +213,7 @@ def tile_crossmultiheadattention_pa_t_kernel(
 
         def mix_first(s):
             b, j = divmod(s, TILES)
-            for o in range(NS):
+            for o in (1, 0, 2):
                 nc.vector.scalar_tensor_tensor(
                     out=acc[(b, o)][:, :, j, :],
                     in0=by_head(s_1[s][:]),

@@ -430,9 +430,10 @@ def tile_crossmultiheadattention_pa_t_kernel(
                 transpose_stream(b2, k)
             if 0 < s < STEPS - 1:
                 project_last(s + 1)
-                spare_terms(s + 1)
             if 0 < s < STEPS - 2:
                 project_first(s + 2)
+            if 0 < s < STEPS - 1:
+                spare_terms(s + 1)
             for b2, cb in across.get(s, []):
                 project_across(b2, (cb,))
                 scale_across(b2, cb)

@@ -67,7 +67,7 @@ def tile_crossmultiheadattention_pa_t_kernel(
         out_pool = ctx.enter_context(tc.tile_pool(name="out", bufs=2))
         misc_ps = ctx.enter_context(tc.psum_pool(name="misc_ps", bufs=3))
         q2_ps = ctx.enter_context(tc.psum_pool(name="q2_ps", bufs=2))
-        f_ps = ctx.enter_context(tc.psum_pool(name="f_ps", bufs=3))
+        f_ps = ctx.enter_context(tc.psum_pool(name="f_ps", bufs=1))
 
         x_raw = {}
         x_grouped = {}
@@ -196,10 +196,13 @@ def tile_crossmultiheadattention_pa_t_kernel(
             project(s, 2, q2)
             q_2[s] = q2
 
+        def mix_order(s):
+            return [(n - s) % NS for n in range(NS)]
+
         def transpose_back(s):
             b, j = divmod(s, TILES)
-            for o in range(NS):
-                bank = f_ps.tile([P, D], F32, tag="f", name="f")
+            for o in mix_order(s - 1):
+                bank = f_ps.tile([P, D], F32, tag="f%d" % o, name="f%d" % o)
                 for cb in range(CB):
                     nc.tensor.transpose(
                         out=bank[:, cb * P : (cb + 1) * P],
@@ -213,7 +216,7 @@ def tile_crossmultiheadattention_pa_t_kernel(
 
         def mix_first(s):
             b, j = divmod(s, TILES)
-            for o in (1, 0, 2):
+            for o in mix_order(s):
                 nc.vector.scalar_tensor_tensor(
                     out=acc[(b, o)][:, :, j, :],
                     in0=by_head(s_1[s][:]),
@@ -263,7 +266,7 @@ def tile_crossmultiheadattention_pa_t_kernel(
                         in1=spare[(b, g)][:, 0 : j1 - j0, :].rearrange("p j (h c) -> p h j c", h=H),
                         op=ADD,
                     )
-            for o in range(NS):
+            for o in mix_order(s):
                 if spare_group(s, o) is not None:
                     continue
                 nc.vector.scalar_tensor_tensor(

@@ -23,12 +23,24 @@ WORDS = D // 2
 CB = D // P
 AHEAD = 3
 
-POOL_F = [(b, c) for b in range(1, NB) for c in (0, 1)]
-GB = 6
-G_FIRST = ()
+POOL_F = {(b, c): 2 for b in range(2, NB) for c in (0, 1)}
+POOL_1 = {(1, 0): 3, (1, 1): 3, (1, 2): 3}
+POOL_0 = (1, 3)
 G_MID = ((2, 0, 2, 1), (1, 0, 1, 1))
 G_LATE = G_MID + ((1, 2, 4, 3), (2, 2, 4, 3))
 G_LAST = ((1, 0, 2, 1), (2, 0, 2, 1), (2, 2, 3, 2))
+GB = 6
+ORDER = "Tx cx X2 X1 c1 sp X0 f0 mf Tb ml q".split()
+ROT = ((0, 1, 2), (2, 0, 1), (1, 2, 0))
+FL1 = (1, 1, 1)
+Q1 = (1, 1, 2)
+A1 = (1, 1, 2, 2)
+FL2 = (2, 3, 4)
+Q2 = (3, 4, 5)
+A2 = (4, 5, 5, 6)
+FOFF = 7
+QO = (6, 5, 4)
+AO = (5, 4, 3, 2)
 
 FLOPS = 2 * NS * NB * S * D * D
 
@@ -70,11 +82,13 @@ def tile_crossmultiheadattention_pa_t_kernel(
         f_ps = ctx.enter_context(tc.psum_pool(name="f_ps", bufs=1))
 
         x_raw = {}
+        x_bank = {}
         x_grouped = {}
         x_codes = {}
         x_scales = {}
         f_t = {}
         q_0 = {}
+        q_1 = {}
         s_1 = {}
         q_2 = {}
         f_bank = {}
@@ -87,15 +101,17 @@ def tile_crossmultiheadattention_pa_t_kernel(
             src = streams[i][b].rearrange("(p j) k -> p (j k)", j=TILES)
             nc.sync.dma_start(out=x_raw[(b, i)][:, cols], in_=src[:, cols])
 
-        def transpose_stream(b, k):
+        def new_bank(where="m"):
+            if where == "m":
+                return misc_ps.tile([P, D], F32, tag="misc", name="misc")
+            if where == "q":
+                return q2_ps.tile([P, D], F32, tag="q2", name="q2")
+            return f_ps.tile([P, D], F32, tag="f" + where, name="f" + where)
+
+        def flip(b, k, where="m"):
             i, half = divmod(k, 2)
             words = x_raw[(b, i)][:].bitcast(F32)
-            if (b, i) not in x_grouped:
-                x_grouped[(b, i)] = grouped_pool.tile(
-                    [P, S * PACK], BF16, tag="grouped", name="grouped", align_bytes=64
-                )
-            grouped_words = x_grouped[(b, i)][:].bitcast(F32)
-            xt = misc_ps.tile([P, 4 * P], F32, tag="misc", name="xt")
+            xt = new_bank(where)
             for jj in range(2):
                 for u in range(2):
                     row = (2 * half + jj) * WORDS
@@ -104,11 +120,20 @@ def tile_crossmultiheadattention_pa_t_kernel(
                         in_=words[:, row + u : row + WORDS : 2],
                         identity=ident[:],
                     )
+            x_bank[(b, k)] = xt
+
+        def group(b, k):
+            i, half = divmod(k, 2)
+            if (b, i) not in x_grouped:
+                x_grouped[(b, i)] = grouped_pool.tile(
+                    [P, S * PACK], BF16, tag="grouped", name="grouped", align_bytes=64
+                )
+            grouped_words = x_grouped[(b, i)][:].bitcast(F32)
             nc.scalar.copy(
                 out=grouped_words[:, half * 4 * P : (half + 1) * 4 * P].rearrange(
                     "q (jj r u) -> q jj r u", jj=2, u=2
                 ),
-                in_=xt[:].rearrange("q (jj u r) -> q jj r u", jj=2, u=2),
+                in_=x_bank[(b, k)][:].rearrange("q (jj u r) -> q jj r u", jj=2, u=2),
             )
 
         def quantise_stream(b, i, tokens=slice(0, S)):
@@ -121,9 +146,9 @@ def tile_crossmultiheadattention_pa_t_kernel(
                 in_=x_grouped[(b, i)][:, tokens.start * PACK : tokens.stop * PACK],
             )
 
-        def project_across(b, blocks, tokens=slice(0, S)):
+        def project_across(b, blocks, tokens=slice(0, S), where="m"):
             n = tokens.stop - tokens.start
-            q0 = misc_ps.tile([P, S], F32, tag="misc", name="q0")
+            q0 = new_bank(where)
             for m, cb in enumerate(blocks):
                 chans = slice(cb * P, (cb + 1) * P)
                 nc.tensor.matmul_mx(
@@ -137,39 +162,50 @@ def tile_crossmultiheadattention_pa_t_kernel(
                 )
                 q_0[(b, cb, tokens.start)] = q0[:, m * n : (m + 1) * n]
 
-        def scale_across(b, cb, tokens=slice(0, S), vector=False):
-            for o in range(NS):
-                if (b, o) not in f_t:
-                    f_t[(b, o)] = ft_pool.tile([P, CB, S], F32, tag="ft%d" % o, name="ft%d" % o)
-                if o > 0 and (b, cb) in POOL_F:
-                    if o == 1:
-                        s0 = s0_pool.tile([P, S], F32, tag="s0", name="s0")
-                        nc.scalar.copy(out=s0[:], in_=q_0[(b, cb, tokens.start)])
-                    nc.gpsimd.tensor_scalar(
-                        out=f_t[(b, o)][:, cb, tokens],
-                        in0=s0[:],
-                        scalar1=w_all[:, o : o + 1],
-                        scalar2=beta[:, NS * cb + o : NS * cb + o + 1],
-                        op0=MULT,
-                        op1=ADD,
-                    )
-                elif vector:
-                    nc.vector.tensor_scalar(
-                        out=f_t[(b, o)][:, cb, tokens],
-                        in0=q_0[(b, cb, tokens.start)],
-                        scalar1=w_all[:, o : o + 1],
-                        scalar2=beta[:, NS * cb + o : NS * cb + o + 1],
-                        op0=MULT,
-                        op1=ADD,
-                    )
-                else:
-                    nc.scalar.activation(
-                        out=f_t[(b, o)][:, cb, tokens],
-                        in_=q_0[(b, cb, tokens.start)],
-                        func=IDENTITY,
-                        bias=beta[:, NS * cb + o : NS * cb + o + 1],
-                        scale=w_all[:, o : o + 1],
-                    )
+        def f_tile(b, o):
+            if (b, o) not in f_t:
+                f_t[(b, o)] = ft_pool.tile([P, CB, S], F32, tag="ft%d" % o, name="ft%d" % o)
+            return f_t[(b, o)]
+
+        def scale_act(b, o, cb, tokens=slice(0, S)):
+            nc.scalar.activation(
+                out=f_tile(b, o)[:, cb, tokens],
+                in_=q_0[(b, cb, tokens.start)],
+                func=IDENTITY,
+                bias=beta[:, NS * cb + o : NS * cb + o + 1],
+                scale=w_all[:, o : o + 1],
+            )
+
+        def scale_dve(b, o, cb, tokens=slice(0, S)):
+            nc.vector.tensor_scalar(
+                out=f_tile(b, o)[:, cb, tokens],
+                in0=q_0[(b, cb, tokens.start)],
+                scalar1=w_all[:, o : o + 1],
+                scalar2=beta[:, NS * cb + o : NS * cb + o + 1],
+                op0=MULT,
+                op1=ADD,
+            )
+
+        def scale_pool(b, which, cb, tokens=slice(0, S)):
+            s0 = s0_pool.tile([P, S], F32, tag="s0", name="s0")
+            n = tokens.stop - tokens.start
+            nc.scalar.copy(out=s0[:, 0:n], in_=q_0[(b, cb, tokens.start)])
+            for o in which:
+                nc.gpsimd.tensor_scalar(
+                    out=f_tile(b, o)[:, cb, tokens],
+                    in0=s0[:, 0:n],
+                    scalar1=w_all[:, o : o + 1],
+                    scalar2=beta[:, NS * cb + o : NS * cb + o + 1],
+                    op0=MULT,
+                    op1=ADD,
+                )
+
+        def scale_across(b, cb):
+            k = POOL_F.get((b, cb), POOL_1.get((b, cb), 0))
+            for o in range(NS - k):
+                scale_act(b, o, cb)
+            if k:
+                scale_pool(b, range(NS - k, NS), cb)
 
         def project(s, i, q):
             b, j = divmod(s, TILES)
@@ -184,11 +220,14 @@ def tile_crossmultiheadattention_pa_t_kernel(
                 stop=True,
             )
 
-        def project_first(s):
-            q1 = misc_ps.tile([P, D], F32, tag="misc", name="q1")
+        def project_first(s, where="m"):
+            q1 = new_bank(where)
             project(s, 1, q1)
+            q_1[s] = q1
+
+        def copy_first(s):
             s1 = s1_pool.tile([P, D], F32, tag="s1", name="s1")
-            nc.scalar.copy(out=s1[:], in_=q1[:])
+            nc.scalar.copy(out=s1[:], in_=q_1[s][:])
             s_1[s] = s1
 
         def project_last(s):
@@ -197,7 +236,7 @@ def tile_crossmultiheadattention_pa_t_kernel(
             q_2[s] = q2
 
         def mix_order(s):
-            return [(n - s) % NS for n in range(NS)]
+            return ROT[s % NS]
 
         def transpose_back(s):
             b, j = divmod(s, TILES)
@@ -216,6 +255,9 @@ def tile_crossmultiheadattention_pa_t_kernel(
 
         def mix_first(s):
             b, j = divmod(s, TILES)
+            if j == 0:
+                for o in range(NS):
+                    acc[(b, o)] = out_pool.tile([P, H, TILES, DH], F32, tag="out%d" % o, name="out%d" % o)
             for o in mix_order(s):
                 nc.vector.scalar_tensor_tensor(
                     out=acc[(b, o)][:, :, j, :],
@@ -228,7 +270,7 @@ def tile_crossmultiheadattention_pa_t_kernel(
 
         def spare_groups(b):
             if b == 0:
-                return G_FIRST
+                return ()
             if b < NB - 2:
                 return G_MID
             return G_LATE if b == NB - 2 else G_LAST
@@ -314,13 +356,13 @@ def tile_crossmultiheadattention_pa_t_kernel(
         second_half = slice(TILES * D // 2, TILES * D)
         load_stream(0, 0, first_half)
         load_weight(0)
+        load_stream(0, 0, second_half)
         load_stream(0, 1, first_half)
         load_weight(1)
-        load_stream(0, 0, second_half)
-        load_stream(0, 1, second_half)
         load_stream(0, 2)
         load_weight(2)
-        for b in range(1, AHEAD):
+        load_stream(0, 1, second_half)
+        for b in range(1, AHEAD + 1):
             for i in range(NS):
                 load_stream(b, i)
 
@@ -339,9 +381,9 @@ def tile_crossmultiheadattention_pa_t_kernel(
                 )
             nc.scalar.copy(out=beta[:], in_=beta_ps[:])
 
-        w_grouped = []
-        w_codes = []
-        w_scales = []
+        w_grouped = {}
+        w_codes = {}
+        w_scales = {}
 
         def group_weight(i):
             grouped = const.tile([P, D, PACK], BF16, name="w_grouped%d" % i, align_bytes=64)
@@ -349,7 +391,7 @@ def tile_crossmultiheadattention_pa_t_kernel(
                 out=grouped[:].rearrange("q (c i) t -> q c t i", i=4),
                 in_=w_raw[i][:].rearrange("q t (c i) -> q c t i", i=4),
             )
-            w_grouped.append(grouped)
+            w_grouped[i] = grouped
 
         def quantise_weight(i):
             codes = const.tile([P, D], U32, name="w_codes%d" % i, align_bytes=64)
@@ -357,8 +399,8 @@ def tile_crossmultiheadattention_pa_t_kernel(
             nc.vector.quantize_mx(
                 out=codes[:].bitcast(FP8X4), scales=scales[:], in_=w_grouped[i][:].rearrange("q n t -> q (n t)")
             )
-            w_codes.append(codes)
-            w_scales.append(scales)
+            w_codes[i] = codes
+            w_scales[i] = scales
 
         ctx.enter_context(
             tc.manual_schedule(
@@ -368,105 +410,148 @@ def tile_crossmultiheadattention_pa_t_kernel(
 
         early = slice(0, S // 2)
         late = slice(S // 2, S)
-        transpose_stream(0, 0)
-        mix_bias()
-        transpose_stream(0, 2)
+        all_blocks = tuple(range(CB))
+
+        def scale_tile(b, j, engine=scale_act):
+            for o in range(NS):
+                for cb in range(CB):
+                    engine(b, o, cb, slice(j * P, (j + 1) * P))
+
+        flip(0, 0)
+        group(0, 0)
         group_weight(0)
         quantise_stream(0, 0, early)
         quantise_weight(0)
-        project_across(0, (0, 2), early)
-        project_across(0, (1, 3), early)
+        mix_bias()
+        flip(0, 1)
+        group(0, 1)
+        flip(0, 2, where="q")
+        group(0, 2)
+        project_across(0, all_blocks, slice(0 * P, 1 * P))
+        scale_tile(0, 0)
+        quantise_stream(0, 0, late)
+        project_across(0, (0, 2), late)
+        project_across(0, (1, 3), late, where="q")
         group_weight(1)
         quantise_stream(0, 1, early)
         quantise_weight(1)
-        scale_across(0, 0, early)
-        scale_across(0, 2, early)
-        scale_across(0, 1, early, vector=True)
-        scale_across(0, 3, early, vector=True)
-        project_first(0)
+        project_across(0, all_blocks, slice(1 * P, 2 * P))
+        flip(0, 4, where="q")
+        project_first(0, where="0")
+        scale_pool(0, range(NS - 3, NS), 0, late)
+        scale_pool(0, range(NS - 3, NS), 2, late)
+        copy_first(0)
+        group_weight(2)
+        quantise_weight(2)
         transpose_back(0)
+        mix_first(0)
+        scale_tile(0, 1)
         project_first(1)
-        for k in (1, 4, 5, 3):
-            transpose_stream(0, k)
+        copy_first(1)
+        group(0, 4)
+        flip(0, 5)
+        group(0, 5)
+        scale_pool(0, range(NS - 3, NS), 1, late)
+        scale_pool(0, range(NS - 3, NS), 3, late)
+        transpose_back(1)
+        mix_first(1)
+        quantise_stream(0, 2)
+        flip(0, 3)
+        group(0, 3)
+        flip(1, 0)
+        group(1, 0)
+        flip(1, 1)
+        group(1, 1)
+        quantise_stream(0, 1, late)
+        quantise_stream(1, 0)
+        flip(1, 2)
+        group(1, 2)
+        flip(1, 3)
+        group(1, 3)
+        project_last(0)
+        project_last(1)
+        mix_last(0)
+        project_first(2)
+        copy_first(2)
+        project_across(1, (0,))
+        scale_across(1, 0)
+        project_first(3)
+        copy_first(3)
+        transpose_back(2)
+        mix_last(1)
+        quantise_stream(1, 1)
+        project_across(1, (1,))
+        scale_across(1, 1)
+        project_last(2)
+        flip(1, 4)
+        group(1, 4)
+        flip(1, 5)
+        group(1, 5)
 
-        across = {
-            1: [(1, 0), (1, 1)],
-            2: [(1, 2), (1, 3)],
-            4: [(2, 0)],
-            5: [(2, 1), (2, 2)],
-            6: [(2, 3)],
-        }
-        flips = {
-            0: [(1, 2), (1, 3)],
-            1: [(1, 4), (1, 5)],
-            2: [(2, 0), (2, 1)],
-            3: [(2, 2), (2, 3)],
-            4: [(2, 4), (2, 5)],
-        }
-        quants = {
-            0: [(1, 0)],
-            1: [(1, 1)],
-            2: [(1, 2)],
-            3: [(2, 0)],
-            4: [(2, 1)],
-            5: [(2, 2)],
-        }
-
-        def plan(table, b, first, per_step, count):
-            for n in range(count):
-                table.setdefault(first + n // per_step, []).append((b, n))
-
+        across = {}
+        flips = {}
+        quants = {}
+        for k in range(2 * NS):
+            if FL1[k // 2] >= 2:
+                flips.setdefault(FL1[k // 2], []).append((1, k))
+        for i in range(NS):
+            if Q1[i] >= 2:
+                quants.setdefault(Q1[i], []).append((1, i))
+        for c in range(CB):
+            if A1[c] >= 2:
+                across.setdefault(A1[c], []).append((1, c))
+        for k in range(2 * NS):
+            flips.setdefault(FL2[k // 2], []).append((2, k))
+        for i in range(NS):
+            quants.setdefault(Q2[i], []).append((2, i))
+        for c in range(CB):
+            across.setdefault(A2[c], []).append((2, c))
         for b in range(3, NB):
-            plan(flips, b, TILES * b - 7, 2, 2 * NS)
-            plan(quants, b, TILES * b - 6, 1, NS)
-            plan(across, b, TILES * b - 5, 1, CB)
+            for k in range(2 * NS):
+                flips.setdefault(TILES * b - FOFF + k // 2, []).append((b, k))
+            for i in range(NS):
+                quants.setdefault(TILES * b - QO[i], []).append((b, i))
+            for c in range(CB):
+                across.setdefault(TILES * b - AO[c], []).append((b, c))
 
-        for s in range(STEPS):
+        for s in range(2, STEPS):
             b, j = divmod(s, TILES)
-            if j == 0:
+            if j == 0 and b:
                 if b + AHEAD < NB:
                     for i in range(NS):
                         load_stream(b + AHEAD, i)
-                for o in range(NS):
-                    acc[(b, o)] = out_pool.tile([P, H, TILES, DH], F32, tag="out%d" % o, name="out%d" % o)
-            for b2, k in flips.get(s, [])[:2] if s else []:
-                transpose_stream(b2, k)
-            if 0 < s < STEPS - 1:
-                project_last(s + 1)
-            if 0 < s < STEPS - 2:
-                project_first(s + 2)
-            if 0 < s < STEPS - 1:
-                spare_terms(s + 1)
-            for b2, cb in across.get(s, []):
-                project_across(b2, (cb,))
-                scale_across(b2, cb)
-            mix_first(s)
-            if s + 1 < STEPS:
-                transpose_back(s + 1)
-            if s == 0:
-                group_weight(2)
-                quantise_stream(0, 0, late)
-                quantise_weight(2)
-                quantise_stream(0, 2)
-                project_across(0, (0, 2), late)
-                project_across(0, (1, 3), late)
-                project_last(0)
-                project_last(1)
-                spare_terms(1)
-                scale_across(0, 0, late)
-                scale_across(0, 2, late)
-                quantise_stream(0, 1, late)
-                project_first(2)
-                transpose_stream(1, 0)
-                transpose_stream(1, 1)
-            for b2, k in flips.get(s, [])[2:] if s else flips[0]:
-                transpose_stream(b2, k)
-            mix_last(s)
-            if s == 0:
-                scale_across(0, 1, late, vector=True)
-                scale_across(0, 3, late, vector=True)
-            for b2, i in quants.get(s, []):
-                quantise_stream(b2, i)
+            for op in ORDER:
+                if op == "Tx":
+                    for b2, k in flips.get(s, []):
+                        flip(b2, k)
+                elif op == "cx":
+                    for b2, k in flips.get(s, []):
+                        group(b2, k)
+                elif op == "TX":
+                    for b2, k in flips.get(s, []):
+                        flip(b2, k)
+                        group(b2, k)
+                elif op == "X2" and s + 1 < STEPS:
+                    project_last(s + 1)
+                elif op == "X1" and s + 2 < STEPS:
+                    project_first(s + 2)
+                elif op == "c1" and s + 2 < STEPS:
+                    copy_first(s + 2)
+                elif op == "sp" and s + 1 < STEPS:
+                    spare_terms(s + 1)
+                elif op == "X0":
+                    for b2, cb in across.get(s, []):
+                        project_across(b2, (cb,))
+                        scale_across(b2, cb)
+                elif op == "mf":
+                    mix_first(s)
+                elif op == "Tb" and s + 1 < STEPS:
+                    transpose_back(s + 1)
+                elif op == "ml":
+                    mix_last(s)
+                elif op == "q":
+                    for b2, i in quants.get(s, []):
+                        quantise_stream(b2, i)
             if b + 1 < NB:
                 if j == TILES - 1:
                     store(b, 0, TILES)

@@ -31,7 +31,7 @@ G_LATE = G_MID + ((1, 2, 4, 3), (2, 2, 4, 3))
 G_LAST = ((1, 0, 2, 1), (2, 0, 2, 1), (2, 2, 3, 2))
 GB = 6
 ORDER = "Tx cx X2 X1 c1 sp X0 f0 mf Tb ml q".split()
-ROT = ((0, 1, 2), (2, 0, 1), (1, 2, 0))
+MFO = (1, 0, 2)
 FL1 = (1, 1, 1)
 Q1 = (1, 1, 2)
 A1 = (1, 1, 2, 2)
@@ -79,7 +79,7 @@ def tile_crossmultiheadattention_pa_t_kernel(
         out_pool = ctx.enter_context(tc.tile_pool(name="out", bufs=2))
         misc_ps = ctx.enter_context(tc.psum_pool(name="misc_ps", bufs=3))
         q2_ps = ctx.enter_context(tc.psum_pool(name="q2_ps", bufs=2))
-        f_ps = ctx.enter_context(tc.psum_pool(name="f_ps", bufs=1))
+        f_ps = ctx.enter_context(tc.psum_pool(name="f_ps", bufs=3))
 
         x_raw = {}
         x_bank = {}
@@ -106,7 +106,7 @@ def tile_crossmultiheadattention_pa_t_kernel(
                 return misc_ps.tile([P, D], F32, tag="misc", name="misc")
             if where == "q":
                 return q2_ps.tile([P, D], F32, tag="q2", name="q2")
-            return f_ps.tile([P, D], F32, tag="f" + where, name="f" + where)
+            return f_ps.tile([P, D], F32, tag="f", name="f")
 
         def flip(b, k, where="m"):
             i, half = divmod(k, 2)
@@ -236,12 +236,12 @@ def tile_crossmultiheadattention_pa_t_kernel(
             q_2[s] = q2
 
         def mix_order(s):
-            return ROT[s % NS]
+            return MFO
 
         def transpose_back(s):
             b, j = divmod(s, TILES)
-            for o in mix_order(s - 1):
-                bank = f_ps.tile([P, D], F32, tag="f%d" % o, name="f%d" % o)
+            for o in range(NS):
+                bank = f_ps.tile([P, D], F32, tag="f", name="f")
                 for cb in range(CB):
                     nc.tensor.transpose(
                         out=bank[:, cb * P : (cb + 1) * P],
@@ -308,7 +308,7 @@ def tile_crossmultiheadattention_pa_t_kernel(
                         in1=spare[(b, g)][:, 0 : j1 - j0, :].rearrange("p j (h c) -> p h j c", h=H),
                         op=ADD,
                     )
-            for o in mix_order(s):
+            for o in range(NS):
                 if spare_group(s, o) is not None:
                     continue
                 nc.vector.scalar_tensor_tensor(

from contextlib import ExitStack

import concourse.mybir as mybir
from concourse.masks import make_identity

F32 = mybir.dt.float32
BF16 = mybir.dt.bfloat16
U32 = mybir.dt.uint32
U8 = mybir.dt.uint8
FP8X4 = mybir.dt.float8_e4m3fn_x4
MULT = mybir.AluOpType.mult
ADD = mybir.AluOpType.add
COPY = mybir.ActivationFunctionType.Copy
IDENTITY = mybir.ActivationFunctionType.Identity

P = 128
PACK = 4
NB, S, D, H, NS = 8, 512, 512, 4, 3
DH = D // H
TILES = S // P
STEPS = NB * TILES
WORDS = D // 2
CB = D // P
AHEAD = 3

POOL_F = {(b, c): 2 for b in range(2, NB) for c in (0, 1)}
POOL_1 = {(1, 0): 3, (1, 1): 3, (1, 2): 3}
POOL_0 = (1, 3)
G_MID = ((2, 0, 2, 1), (1, 0, 1, 1))
G_LATE = G_MID + ((1, 2, 4, 3), (2, 2, 4, 3))
G_LAST = ((1, 0, 2, 1), (2, 0, 2, 1), (2, 2, 3, 2))
GB = 6
ORDER = "Tx cx X2 X1 c1 sp X0 f0 mf Tb ml q".split()
MFO = (1, 0, 2)
FL1 = (1, 1, 1)
Q1 = (1, 1, 2)
A1 = (1, 1, 2, 2)
FL2 = (2, 3, 4)
Q2 = (3, 4, 5)
A2 = (4, 5, 5, 6)
FOFF = 7
QO = (6, 5, 4)
AO = (5, 4, 3, 2)

FLOPS = 2 * NS * NB * S * D * D


def tile_crossmultiheadattention_pa_t_kernel(
    tc,
    input_tensor,
    position_embedding,
    attr,
    Wq,
    bq,
    Wqp,
    bqp,
    Wqa,
    bqa,
    w_matrix,
    out_0,
    out_1,
    out_2,
):
    nc = tc.nc
    streams = (input_tensor, position_embedding, attr)
    weights = (Wq, Wqp, Wqa)
    biases = (bq, bqp, bqa)
    outs = (out_0, out_1, out_2)

    with ExitStack() as ctx:
        const = ctx.enter_context(tc.tile_pool(name="const", bufs=1))
        x_pool = ctx.enter_context(tc.tile_pool(name="x", bufs=AHEAD))
        grouped_pool = ctx.enter_context(tc.tile_pool(name="grouped", bufs=NS))
        mx_pool = ctx.enter_context(tc.tile_pool(name="mx", bufs=3))
        ft_pool = ctx.enter_context(tc.tile_pool(name="ft", bufs=2))
        s1_pool = ctx.enter_context(tc.tile_pool(name="s1", bufs=3))
        s0_pool = ctx.enter_context(tc.tile_pool(name="s0", bufs=3))
        g_pool = ctx.enter_context(tc.tile_pool(name="g", bufs=GB))
        out_pool = ctx.enter_context(tc.tile_pool(name="out", bufs=2))
        misc_ps = ctx.enter_context(tc.psum_pool(name="misc_ps", bufs=3))
        q2_ps = ctx.enter_context(tc.psum_pool(name="q2_ps", bufs=2))
        f_ps = ctx.enter_context(tc.psum_pool(name="f_ps", bufs=3))

        x_raw = {}
        x_bank = {}
        x_grouped = {}
        x_codes = {}
        x_scales = {}
        f_t = {}
        q_0 = {}
        q_1 = {}
        s_1 = {}
        q_2 = {}
        f_bank = {}
        acc = {}
        spare = {}

        def load_stream(b, i, cols=slice(0, TILES * D)):
            if (b, i) not in x_raw:
                x_raw[(b, i)] = x_pool.tile([P, TILES * D], BF16, tag="x%d" % i, name="x%d" % i)
            src = streams[i][b].rearrange("(p j) k -> p (j k)", j=TILES)
            nc.sync.dma_start(out=x_raw[(b, i)][:, cols], in_=src[:, cols])

        def new_bank(where="m"):
            if where == "m":
                return misc_ps.tile([P, D], F32, tag="misc", name="misc")
            if where == "q":
                return q2_ps.tile([P, D], F32, tag="q2", name="q2")
            return f_ps.tile([P, D], F32, tag="f", name="f")

        def flip(b, k, where="m"):
            i, half = divmod(k, 2)
            words = x_raw[(b, i)][:].bitcast(F32)
            xt = new_bank(where)
            for jj in range(2):
                for u in range(2):
                    row = (2 * half + jj) * WORDS
                    nc.tensor.transpose(
                        out=xt[:, (2 * jj + u) * P : (2 * jj + u + 1) * P],
                        in_=words[:, row + u : row + WORDS : 2],
                        identity=ident[:],
                    )
            x_bank[(b, k)] = xt

        def group(b, k):
            i, half = divmod(k, 2)
            if (b, i) not in x_grouped:
                x_grouped[(b, i)] = grouped_pool.tile(
                    [P, S * PACK], BF16, tag="grouped", name="grouped", align_bytes=64
                )
            grouped_words = x_grouped[(b, i)][:].bitcast(F32)
            nc.scalar.copy(
                out=grouped_words[:, half * 4 * P : (half + 1) * 4 * P].rearrange(
                    "q (jj r u) -> q jj r u", jj=2, u=2
                ),
                in_=x_bank[(b, k)][:].rearrange("q (jj u r) -> q jj r u", jj=2, u=2),
            )

        def quantise_stream(b, i, tokens=slice(0, S)):
            if (b, i) not in x_codes:
                x_codes[(b, i)] = mx_pool.tile([P, S], U32, tag="codes%d" % i, name="codes%d" % i, align_bytes=64)
                x_scales[(b, i)] = mx_pool.tile([P, S], U8, tag="scales%d" % i, name="scales%d" % i, align_bytes=64)
            nc.vector.quantize_mx(
                out=x_codes[(b, i)][:, tokens].bitcast(FP8X4),
                scales=x_scales[(b, i)][:, tokens],
                in_=x_grouped[(b, i)][:, tokens.start * PACK : tokens.stop * PACK],
            )

        def project_across(b, blocks, tokens=slice(0, S), where="m"):
            n = tokens.stop - tokens.start
            q0 = new_bank(where)
            for m, cb in enumerate(blocks):
                chans = slice(cb * P, (cb + 1) * P)
                nc.tensor.matmul_mx(
                    out=q0[:, m * n : (m + 1) * n],
                    lhsT=w_codes[0][:, chans].bitcast(FP8X4),
                    lhsT_scale=w_scales[0][:, chans],
                    rhs=x_codes[(b, 0)][:, tokens].bitcast(FP8X4),
                    rhs_scale=x_scales[(b, 0)][:, tokens],
                    start=True,
                    stop=True,
                )
                q_0[(b, cb, tokens.start)] = q0[:, m * n : (m + 1) * n]

        def f_tile(b, o):
            if (b, o) not in f_t:
                f_t[(b, o)] = ft_pool.tile([P, CB, S], F32, tag="ft%d" % o, name="ft%d" % o)
            return f_t[(b, o)]

        def scale_act(b, o, cb, tokens=slice(0, S)):
            nc.scalar.activation(
                out=f_tile(b, o)[:, cb, tokens],
                in_=q_0[(b, cb, tokens.start)],
                func=IDENTITY,
                bias=beta[:, NS * cb + o : NS * cb + o + 1],
                scale=w_all[:, o : o + 1],
            )

        def scale_dve(b, o, cb, tokens=slice(0, S)):
            nc.vector.tensor_scalar(
                out=f_tile(b, o)[:, cb, tokens],
                in0=q_0[(b, cb, tokens.start)],
                scalar1=w_all[:, o : o + 1],
                scalar2=beta[:, NS * cb + o : NS * cb + o + 1],
                op0=MULT,
                op1=ADD,
            )

        def scale_pool(b, which, cb, tokens=slice(0, S)):
            s0 = s0_pool.tile([P, S], F32, tag="s0", name="s0")
            n = tokens.stop - tokens.start
            nc.scalar.copy(out=s0[:, 0:n], in_=q_0[(b, cb, tokens.start)])
            for o in which:
                nc.gpsimd.tensor_scalar(
                    out=f_tile(b, o)[:, cb, tokens],
                    in0=s0[:, 0:n],
                    scalar1=w_all[:, o : o + 1],
                    scalar2=beta[:, NS * cb + o : NS * cb + o + 1],
                    op0=MULT,
                    op1=ADD,
                )

        def scale_across(b, cb):
            k = POOL_F.get((b, cb), POOL_1.get((b, cb), 0))
            for o in range(NS - k):
                scale_act(b, o, cb)
            if k:
                scale_pool(b, range(NS - k, NS), cb)

        def project(s, i, q):
            b, j = divmod(s, TILES)
            tokens = slice(j * P, (j + 1) * P)
            nc.tensor.matmul_mx(
                out=q[:],
                lhsT=x_codes[(b, i)][:, tokens].bitcast(FP8X4),
                lhsT_scale=x_scales[(b, i)][:, tokens],
                rhs=w_codes[i][:].bitcast(FP8X4),
                rhs_scale=w_scales[i][:],
                start=True,
                stop=True,
            )

        def project_first(s, where="m"):
            q1 = new_bank(where)
            project(s, 1, q1)
            q_1[s] = q1

        def copy_first(s):
            s1 = s1_pool.tile([P, D], F32, tag="s1", name="s1")
            nc.scalar.copy(out=s1[:], in_=q_1[s][:])
            s_1[s] = s1

        def project_last(s):
            q2 = q2_ps.tile([P, D], F32, tag="q2", name="q2")
            project(s, 2, q2)
            q_2[s] = q2

        def mix_order(s):
            return MFO

        def transpose_back(s):
            b, j = divmod(s, TILES)
            for o in range(NS):
                bank = f_ps.tile([P, D], F32, tag="f", name="f")
                for cb in range(CB):
                    nc.tensor.transpose(
                        out=bank[:, cb * P : (cb + 1) * P],
                        in_=f_t[(b, o)][:, cb, j * P : (j + 1) * P],
                        identity=ident[:],
                    )
                f_bank[(s, o)] = bank

        def by_head(ap):
            return ap.rearrange("p (h c) -> p h c", h=H)

        def mix_first(s):
            b, j = divmod(s, TILES)
            if j == 0:
                for o in range(NS):
                    acc[(b, o)] = out_pool.tile([P, H, TILES, DH], F32, tag="out%d" % o, name="out%d" % o)
            for o in mix_order(s):
                nc.vector.scalar_tensor_tensor(
                    out=acc[(b, o)][:, :, j, :],
                    in0=by_head(s_1[s][:]),
                    scalar=w_all[:, NS + o : NS + o + 1],
                    in1=by_head(f_bank[(s, o)][:]),
                    op0=MULT,
                    op1=ADD,
                )

        def spare_groups(b):
            if b == 0:
                return ()
            if b < NB - 2:
                return G_MID
            return G_LATE if b == NB - 2 else G_LAST

        def spare_group(s, o):
            b, j = divmod(s, TILES)
            for g in spare_groups(b):
                if g[0] == o and g[1] <= j < g[2]:
                    return g
            return None

        def spare_terms(s):
            b, j = divmod(s, TILES)
            for o in range(NS):
                g = spare_group(s, o)
                if g is None:
                    continue
                if j == g[1]:
                    spare[(b, g)] = g_pool.tile([P, 2, D], F32, tag="g", name="g")
                nc.scalar.activation(
                    out=spare[(b, g)][:, j - g[1], :],
                    in_=q_2[s][:],
                    func=COPY,
                    scale=w_all[:, 2 * NS + o : 2 * NS + o + 1],
                )

        def mix_last(s):
            b, j = divmod(s, TILES)
            for g in spare_groups(b):
                if g[3] == j:
                    o, j0, j1 = g[:3]
                    nc.gpsimd.tensor_tensor(
                        out=acc[(b, o)][:, :, j0:j1, :],
                        in0=acc[(b, o)][:, :, j0:j1, :],
                        in1=spare[(b, g)][:, 0 : j1 - j0, :].rearrange("p j (h c) -> p h j c", h=H),
                        op=ADD,
                    )
            for o in range(NS):
                if spare_group(s, o) is not None:
                    continue
                nc.vector.scalar_tensor_tensor(
                    out=acc[(b, o)][:, :, j, :],
                    in0=by_head(q_2[s][:]),
                    scalar=w_all[:, 2 * NS + o : 2 * NS + o + 1],
                    in1=acc[(b, o)][:, :, j, :],
                    op0=MULT,
                    op1=ADD,
                )

        def store(b, j0, j1):
            for o in range(NS):
                nc.sync.dma_start(
                    out=outs[o][b].rearrange("h (p j) c -> p h j c", j=TILES)[:, :, j0:j1, :],
                    in_=acc[(b, o)][:, :, j0:j1, :],
                )

        ident = const.tile([P, P], F32, name="ident")
        make_identity(nc, ident[:])

        w_bf = const.tile([P, NS * NS], BF16, name="w_bf")
        nc.scalar.dma_start(out=w_bf[:], in_=w_matrix.rearrange("i o -> (i o)").partition_broadcast(P))
        w_all = const.tile([P, NS * NS], F32, name="w_all")

        w_rows = const.tile([P, NS], BF16, name="w_rows")
        nc.vector.memset(w_rows[:], 0.0)
        nc.scalar.dma_start(out=w_rows[0:NS, :], in_=w_matrix)
        bias_rows = const.tile([P, D], BF16, name="bias_rows")
        nc.vector.memset(bias_rows[:], 0.0)
        for i in range(NS):
            nc.scalar.dma_start(out=bias_rows[i : i + 1, :], in_=biases[i].rearrange("(o c) -> o c", o=1))

        w_raw = []

        def load_weight(i):
            raw = const.tile([P, PACK, D], BF16, name="w_raw%d" % i)
            nc.sync.dma_start(
                out=raw[:].rearrange("q t n -> q (t n)"),
                in_=weights[i].rearrange("(q t) n -> q (t n)", t=PACK),
            )
            w_raw.append(raw)

        first_half = slice(0, TILES * D // 2)
        second_half = slice(TILES * D // 2, TILES * D)
        load_stream(0, 0, first_half)
        load_weight(0)
        load_stream(0, 0, second_half)
        load_stream(0, 1, first_half)
        load_weight(1)
        load_stream(0, 2)
        load_weight(2)
        load_stream(0, 1, second_half)
        for b in range(1, AHEAD + 1):
            for i in range(NS):
                load_stream(b, i)

        nc.vector.tensor_copy(out=w_all[:], in_=w_bf[:])
        beta = const.tile([P, CB * NS], F32, name="beta")

        def mix_bias():
            beta_ps = misc_ps.tile([P, CB * NS], F32, tag="misc", name="beta_ps")
            for cb in range(CB):
                nc.tensor.matmul(
                    out=beta_ps[:, NS * cb : NS * (cb + 1)],
                    lhsT=bias_rows[:, cb * P : (cb + 1) * P],
                    rhs=w_rows[:],
                    start=True,
                    stop=True,
                )
            nc.scalar.copy(out=beta[:], in_=beta_ps[:])

        w_grouped = {}
        w_codes = {}
        w_scales = {}

        def group_weight(i):
            grouped = const.tile([P, D, PACK], BF16, name="w_grouped%d" % i, align_bytes=64)
            nc.vector.tensor_copy(
                out=grouped[:].rearrange("q (c i) t -> q c t i", i=4),
                in_=w_raw[i][:].rearrange("q t (c i) -> q c t i", i=4),
            )
            w_grouped[i] = grouped

        def quantise_weight(i):
            codes = const.tile([P, D], U32, name="w_codes%d" % i, align_bytes=64)
            scales = const.tile([P, D], U8, name="w_scales%d" % i, align_bytes=64)
            nc.vector.quantize_mx(
                out=codes[:].bitcast(FP8X4), scales=scales[:], in_=w_grouped[i][:].rearrange("q n t -> q (n t)")
            )
            w_codes[i] = codes
            w_scales[i] = scales

        ctx.enter_context(
            tc.manual_schedule(
                engines={mybir.EngineType.PE, mybir.EngineType.Activation, mybir.EngineType.DVE}
            )
        )

        early = slice(0, S // 2)
        late = slice(S // 2, S)
        all_blocks = tuple(range(CB))

        def scale_tile(b, j, engine=scale_act):
            for o in range(NS):
                for cb in range(CB):
                    engine(b, o, cb, slice(j * P, (j + 1) * P))

        flip(0, 0)
        group(0, 0)
        group_weight(0)
        quantise_stream(0, 0, early)
        quantise_weight(0)
        mix_bias()
        flip(0, 1)
        group(0, 1)
        flip(0, 2, where="q")
        group(0, 2)
        project_across(0, all_blocks, slice(0 * P, 1 * P))
        scale_tile(0, 0)
        quantise_stream(0, 0, late)
        project_across(0, (0, 2), late)
        project_across(0, (1, 3), late, where="q")
        group_weight(1)
        quantise_stream(0, 1, early)
        quantise_weight(1)
        project_across(0, all_blocks, slice(1 * P, 2 * P))
        flip(0, 4, where="q")
        project_first(0, where="0")
        scale_pool(0, range(NS - 3, NS), 0, late)
        scale_pool(0, range(NS - 3, NS), 2, late)
        copy_first(0)
        group_weight(2)
        quantise_weight(2)
        transpose_back(0)
        mix_first(0)
        scale_tile(0, 1)
        project_first(1)
        copy_first(1)
        group(0, 4)
        flip(0, 5)
        group(0, 5)
        scale_pool(0, range(NS - 3, NS), 1, late)
        scale_pool(0, range(NS - 3, NS), 3, late)
        transpose_back(1)
        mix_first(1)
        quantise_stream(0, 2)
        flip(0, 3)
        group(0, 3)
        flip(1, 0)
        group(1, 0)
        flip(1, 1)
        group(1, 1)
        quantise_stream(0, 1, late)
        quantise_stream(1, 0)
        flip(1, 2)
        group(1, 2)
        flip(1, 3)
        group(1, 3)
        project_last(0)
        project_last(1)
        mix_last(0)
        project_first(2)
        copy_first(2)
        project_across(1, (0,))
        scale_across(1, 0)
        project_first(3)
        copy_first(3)
        transpose_back(2)
        mix_last(1)
        quantise_stream(1, 1)
        project_across(1, (1,))
        scale_across(1, 1)
        project_last(2)
        flip(1, 4)
        group(1, 4)
        flip(1, 5)
        group(1, 5)

        across = {}
        flips = {}
        quants = {}
        for k in range(2 * NS):
            if FL1[k // 2] >= 2:
                flips.setdefault(FL1[k // 2], []).append((1, k))
        for i in range(NS):
            if Q1[i] >= 2:
                quants.setdefault(Q1[i], []).append((1, i))
        for c in range(CB):
            if A1[c] >= 2:
                across.setdefault(A1[c], []).append((1, c))
        for k in range(2 * NS):
            flips.setdefault(FL2[k // 2], []).append((2, k))
        for i in range(NS):
            quants.setdefault(Q2[i], []).append((2, i))
        for c in range(CB):
            across.setdefault(A2[c], []).append((2, c))
        for b in range(3, NB):
            for k in range(2 * NS):
                flips.setdefault(TILES * b - FOFF + k // 2, []).append((b, k))
            for i in range(NS):
                quants.setdefault(TILES * b - QO[i], []).append((b, i))
            for c in range(CB):
                across.setdefault(TILES * b - AO[c], []).append((b, c))

        for s in range(2, STEPS):
            b, j = divmod(s, TILES)
            if j == 0 and b:
                if b + AHEAD < NB:
                    for i in range(NS):
                        load_stream(b + AHEAD, i)
            for op in ORDER:
                if op == "Tx":
                    for b2, k in flips.get(s, []):
                        flip(b2, k)
                elif op == "cx":
                    for b2, k in flips.get(s, []):
                        group(b2, k)
                elif op == "TX":
                    for b2, k in flips.get(s, []):
                        flip(b2, k)
                        group(b2, k)
                elif op == "X2" and s + 1 < STEPS:
                    project_last(s + 1)
                elif op == "X1" and s + 2 < STEPS:
                    project_first(s + 2)
                elif op == "c1" and s + 2 < STEPS:
                    copy_first(s + 2)
                elif op == "sp" and s + 1 < STEPS:
                    spare_terms(s + 1)
                elif op == "X0":
                    for b2, cb in across.get(s, []):
                        project_across(b2, (cb,))
                        scale_across(b2, cb)
                elif op == "mf":
                    mix_first(s)
                elif op == "Tb" and s + 1 < STEPS:
                    transpose_back(s + 1)
                elif op == "ml":
                    mix_last(s)
                elif op == "q":
                    for b2, i in quants.get(s, []):
                        quantise_stream(b2, i)
            if b + 1 < NB:
                if j == TILES - 1:
                    store(b, 0, TILES)
            elif j == 1:
                store(b, 0, 2)
            elif j >= 2:
                store(b, j, j + 1)
